import numpy as np
import ml_dtypes


def mxq(x, axis, fmt="e4m3"):
    dtype, down = {"e4m3": (ml_dtypes.float8_e4m3fn, 7), "e5m2": (ml_dtypes.float8_e5m2, 14)}[fmt]
    v = np.moveaxis(np.asarray(x, np.float32).astype(ml_dtypes.bfloat16).astype(np.float64), axis, -1)
    blocks = v.reshape(v.shape[:-1] + (-1, 32))
    amax = np.abs(blocks).max(-1, keepdims=True)
    byte = np.maximum(np.where(amax > 0, np.frexp(amax)[1] - 1 + 127, 0) - down, 1)
    scale = np.exp2(byte - 127.0)
    codes = (blocks / scale).astype(np.float32).astype(dtype).astype(np.float64)
    return np.moveaxis((codes * scale).reshape(v.shape), -1, axis)


WIDE = False


def mx_kscale(k):
    if not WIDE:
        return np.ones(k)
    levels = np.array([10, -10, 5, -5, 0])
    if k % 512:
        return np.exp2(np.random.permutation(np.resize(levels, k // 32))).repeat(32)
    a = np.empty((k // 512, 16))
    for p in range(k // 512):
        a[p, :8] = np.random.permutation(np.resize(levels, 8))
        for g in range(8):
            far = levels[np.abs(levels - a[p, g]) >= 10]
            a[p, g + 8] = far[np.random.randint(len(far))]
    return np.exp2(a.ravel()).repeat(32)


BF16 = ml_dtypes.bfloat16


def bf(x):
    return np.asarray(x, np.float32).astype(BF16)


def f64(x):
    return np.asarray(x).astype(np.float64)


B, S, D, NH = 2, 512, 1024, 8
SCALE = np.sqrt(D // NH)


def draw0():
    s, t = mx_kscale(D), mx_kscale(D)
    return {"x": bf(np.random.standard_normal((B, S, D)) * s),
            "wq": bf(np.random.standard_normal((D, D)) * 0.84 / np.sqrt(D) / s[None, :] * t[:, None]),
            "wk": bf(np.random.standard_normal((D, D)) * 0.84 / np.sqrt(D) / s[None, :] / t[:, None])}


def core(x, wq, wk):
    xq = mxq(f64(x), 2, "e4m3")
    q = xq @ mxq(f64(wq), 1, "e4m3").T
    k = xq @ mxq(f64(wk), 1, "e4m3").T
    sc = (mxq(q, 2, "e4m3") @ mxq(k, 2, "e4m3").transpose(0, 2, 1)) / SCALE
    e = np.exp(sc - sc.max(-1, keepdims=True))
    return e / e.sum(-1, keepdims=True)


def e4m3fn_bytes(y):
    return np.clip(np.asarray(y, np.float64), -448.0, 448.0).astype(np.float32).astype(ml_dtypes.float8_e4m3fn).view(np.uint8)


def e4m3fn_values(b):
    return np.asarray(b, np.uint8).view(ml_dtypes.float8_e4m3fn).astype(np.float64)


def setup_inputs():
    d = draw0()
    x0 = np.asarray(d['x']).astype(np.float64)
    s = (np.max(np.abs(x0), axis=(0, 1), keepdims=True) / 448.0).astype(np.float32)
    out = {}
    for k, v in d.items():
        if k == 'x':
            out['x_bytes'] = e4m3fn_bytes(x0 / s.astype(np.float64))
            out['x_scale'] = s
        else:
            out[k] = v
    return out


def reference(x_bytes, x_scale, wq, wk):
    return core(e4m3fn_values(x_bytes) * x_scale.astype(np.float64), wq, wk)

@@ -1,0 +1,346 @@
+from contextlib import ExitStack
+
+import concourse.mybir as mybir
+from concourse.masks import make_identity
+
+B, S, D = 2, 512, 1024
+SCALE = 128.0 ** -0.5
+FLOPS = 2 * 2 * B * S * D * D + 2 * B * S * S * D
+
+F32 = mybir.dt.float32
+BF16 = mybir.dt.bfloat16
+U32 = mybir.dt.uint32
+U8 = mybir.dt.uint8
+FP8 = mybir.dt.float8_e4m3fn
+FP8X4 = mybir.dt.float8_e4m3fn_x4
+ALU = mybir.AluOpType
+ACT = mybir.ActivationFunctionType
+
+P = 128
+G = 2
+T = 4
+J = 4
+F = 2
+
+
+def tile_attentionnet_pa_kernel(tc, x_bytes, x_scale, wq, wk, out):
+    nc = tc.nc
+    with ExitStack() as ctx:
+        keep = ctx.enter_context(tc.tile_pool(name="keep", bufs=1))
+        wgrp = ctx.enter_context(tc.tile_pool(name="wgrp", bufs=2))
+        stage = ctx.enter_context(tc.tile_pool(name="stage", bufs=3))
+        soft = ctx.enter_context(tc.tile_pool(name="soft", bufs=4))
+        psum = ctx.enter_context(tc.psum_pool(name="psum", bufs=8))
+
+        xs = keep.tile([P, G, 2, 2], F32, name="xs")
+        xraw = [keep.tile([P, J, D], U8, name=f"xraw{b}") for b in range(B)]
+        wraw = {}
+        for m in range(2):
+            for f in range(F):
+                wraw[m, f] = keep.tile([P, T, D], BF16, name=f"wraw{m}{f}", align_bytes=64)
+
+        def load_x(b, js):
+            nc.sync.dma_start(out=xraw[b][:, js, :], in_=x_bytes[b].rearrange("(r j) k -> r j k", j=J)[:, js, :])
+
+        def load_xs():
+            nc.sync.dma_start(out=xs[:].rearrange("p g u e -> p g (u e)"), in_=x_scale.rearrange("o i (g p t) -> p (o i g) t", g=G, t=T))
+
+        def load_w(m, f, h):
+            rows = (wk, wq)[m][f * 512:(f + 1) * 512, :].rearrange("(m t) k -> m t k", t=T)
+            nc.sync.dma_start(out=wraw[m, f][:, 2 * h:2 * h + 2, :], in_=rows[:, 2 * h:2 * h + 2, :])
+
+        load_x(0, slice(0, 2))
+        load_xs()
+        load_w(0, 0, 0)
+        load_w(0, 0, 1)
+        load_x(0, slice(2, 4))
+        for m, f in ((0, 1), (1, 0)):
+            for h in range(2):
+                load_w(m, f, h)
+        load_x(1, slice(0, 4))
+        for h in range(2):
+            load_w(1, 1, h)
+
+        ident = keep.tile([P, P], F32, name="ident")
+        make_identity(nc, ident[:])
+        warm = keep.tile([P, 1], F32, name="warm")
+        nc.vector.memset(warm[:], 0.0)
+        nc.scalar.activation(out=warm[:], in_=warm[:], func=ACT.Exp)
+        zero = keep.tile([P, 512], BF16, name="zero")
+        nc.vector.memset(zero[:], 0.0)
+        one = keep.tile([P, 1], F32, name="one")
+        nc.vector.memset(one[:], 1.0)
+
+        xw, xg = {}, {}
+        xc, xp = {}, {}
+        for b in range(B):
+            xc[b] = keep.tile([P, J, G, P], U32, name=f"xc{b}", align_bytes=64)
+            xp[b] = keep.tile([P, J, G, P], U8, name=f"xp{b}", align_bytes=64)
+        wc, wp = {}, {}
+        for m in range(2):
+            for f in range(F):
+                wc[m, f] = keep.tile([P, T, G, P], U32, name=f"wc{m}{f}", align_bytes=64)
+                wp[m, f] = keep.tile([P, T, G, P], U8, name=f"wp{m}{f}", align_bytes=64)
+        kc, kp = {}, {}
+        for b in range(B):
+            kc[b] = keep.tile([P, F, J, P], U32, name=f"kc{b}", align_bytes=64)
+            kp[b] = keep.tile([P, F, J, P], U8, name=f"kp{b}", align_bytes=64)
+
+        def transposes(views):
+            bank = psum.tile([P, G, 2, P], F32, name="bank", tag="bank")
+            for g in range(G):
+                for u in range(2):
+                    nc.tensor.transpose(bank[:, g, u, :], views[g][u], ident[:])
+            return bank
+
+        def widen_v(b, j):
+            t = stage.tile([P, G, 2, P, 2], BF16, name="xwide", tag="xwide", bufs=4, align_bytes=64)
+            for g in range(G):
+                nc.vector.tensor_scalar(out=t[:, g].rearrange("r u p e -> r p u e"),
+                                        in0=xraw[b][:, j, g * 512:(g + 1) * 512].bitcast(FP8).rearrange("r (p u e) -> r p u e", u=2, e=2),
+                                        scalar1=one[:], scalar2=None, op0=ALU.mult)
+            xw[b, j] = [[t[:, g, u].rearrange("r p e -> r (p e)").bitcast(F32) for u in range(2)] for g in range(G)]
+
+        def every_second(words):
+            return [[words[:, 256 * g + u:256 * (g + 1):2] for u in range(2)] for g in range(G)]
+
+        def widen_s(b, j):
+            t = stage.tile([P, D], BF16, name="xwide", tag="xwide", bufs=4, align_bytes=64)
+            nc.scalar.copy(out=t[:], in_=xraw[b][:, j, :].bitcast(FP8))
+            xw[b, j] = every_second(t[:].bitcast(F32))
+
+        xbank = {}
+
+        def x_turn(b, j):
+            xbank[b, j] = transposes(xw[b, j])
+
+        def x_scale_out(b, j):
+            bank = xbank[b, j]
+            grp = stage.tile([P, G, P, T], BF16, name="xgrp", tag="xgrp", bufs=4, align_bytes=64)
+            for g in range(G):
+                nc.vector.tensor_tensor(
+                    out=grp[:, g].rearrange("p r (u e) -> p r u e", u=2),
+                    in0=bank[:, g].bitcast(BF16).rearrange("p u (r e) -> p r u e", e=2),
+                    in1=xs[:, g].unsqueeze(1).to_broadcast([P, P, 2, 2]),
+                    op=ALU.mult)
+            xg[b, j] = grp
+
+        def x_quant(b, j):
+            grp = xg[b, j]
+            nc.vector.quantize_mx(
+                out=xc[b][:, j].rearrange("p g r -> p (g r)").bitcast(FP8X4),
+                scales=xp[b][:, j].rearrange("p g r -> p (g r)"),
+                in_=grp[:].rearrange("p g r t -> p (g r t)"))
+
+        wg = {}
+
+        def w_slot(m, f, s):
+            if s == 0:
+                wg[m, f] = wgrp.tile([P, T, G, P, T], BF16, name="wgrp_t", tag="wgrp_t", align_bytes=64)
+            bank = transposes(every_second(wraw[m, f][:, s, :].bitcast(F32)))
+            nc.scalar.copy(out=wg[m, f][:, s].bitcast(F32), in_=bank[:].rearrange("p g u r -> p g r u"))
+
+        def w_quant(m, f, h):
+                sl = slice(2 * h, 2 * h + 2)
+                nc.vector.quantize_mx(
+                    out=wc[m, f][:, sl].rearrange("p s g r -> p (s g r)").bitcast(FP8X4),
+                    scales=wp[m, f][:, sl].rearrange("p s g r -> p (s g r)"),
+                    in_=wg[m, f][:, sl].rearrange("p s g r t -> p (s g r t)"))
+
+        def project(m, f, b, j, dst, vector):
+            bank = psum.tile([P, T, P], F32, name="bank", tag="bank")
+            for t in range(T):
+                for g in range(G):
+                    nc.tensor.matmul_mx(
+                        out=bank[:, t, :],
+                        lhsT=wc[m, f][:, t, g, :].bitcast(FP8X4), lhsT_scale=wp[m, f][:, t, g, :],
+                        rhs=xc[b][:, j, g, :].bitcast(FP8X4), rhs_scale=xp[b][:, j, g, :],
+                        start=(g == 0), stop=(g == G - 1))
+            if vector:
+                nc.vector.tensor_copy(out=dst, in_=bank[:].rearrange("p t n -> p n t"))
+            else:
+                nc.scalar.copy(out=dst, in_=bank[:].rearrange("p t n -> p n t"))
+
+        kg = {}
+
+        def k_proj(b, f, j, vector=False):
+            if j % 2 == 0:
+                kg[b, f, j // 2] = stage.tile([P, 2, P, T], BF16, name="kgrp", tag="kgrp", bufs=4, align_bytes=64)
+            project(0, f, b, j, kg[b, f, j // 2][:, j % 2], vector)
+
+        def k_quant(b, f, h):
+            sl = slice(2 * h, 2 * h + 2)
+            nc.vector.quantize_mx(
+                out=kc[b][:, f, sl].rearrange("p j r -> p (j r)").bitcast(FP8X4),
+                scales=kp[b][:, f, sl].rearrange("p j r -> p (j r)"),
+                in_=kg[b, f, h][:].rearrange("p j r t -> p (j r t)"))
+
+        qc, qg = {}, {}
+        sbank, nbias, e, tot, inv = {}, {}, {}, {}, {}
+
+        def q_proj(b, f, j, vector=False):
+            if (b, j) not in qg:
+                qg[b, j] = stage.tile([P, F, P, T], BF16, name="qgrp", tag="qgrp", bufs=5, align_bytes=64)
+            project(1, f, b, j, qg[b, j][:, f], vector)
+
+        def q_quant(b, j):
+            grp = qg[b, j]
+            c = stage.tile([P, F, P], U32, name="qcode", tag="qcode", bufs=6, align_bytes=64)
+            p = stage.tile([P, F, P], U8, name="qplane", tag="qplane", bufs=6, align_bytes=64)
+            nc.vector.quantize_mx(
+                out=c[:].rearrange("p f r -> p (f r)").bitcast(FP8X4),
+                scales=p[:].rearrange("p f r -> p (f r)"),
+                in_=grp[:].rearrange("p f r t -> p (f r t)"))
+            qc[b, j] = (c, p)
+
+        def scores(b, j):
+            c, p = qc[b, j]
+            bank = psum.tile([P, J, P], F32, name="bank", tag="bank")
+            for f in range(F):
+                nc.tensor.matmul_mx(
+                    out=bank[:].rearrange("p j r -> p (j r)"),
+                    lhsT=c[:, f, :].bitcast(FP8X4), lhsT_scale=p[:, f, :],
+                    rhs=kc[b][:, f].rearrange("p j r -> p (j r)").bitcast(FP8X4),
+                    rhs_scale=kp[b][:, f].rearrange("p j r -> p (j r)"),
+                    start=(f == 0), stop=(f == F - 1))
+            sbank[b, j] = bank
+
+        def row_bias(b, j):
+            nbias[b, j] = soft.tile([P, 1], F32, name="nbias")
+            scratch = soft.tile([P, S], F32, name="scratch")
+            nc.vector.tensor_scalar(out=scratch[:], in0=sbank[b, j][:].rearrange("p j r -> p (j r)"), scalar1=-SCALE, scalar2=None,
+                                    op0=ALU.mult, op1=ALU.min, accum_out=nbias[b, j][:])
+
+        def row_exp(b, j):
+            e[b, j] = soft.tile([P, P, J], F32, name="e")
+            tot[b, j] = soft.tile([P, 1], F32, name="tot")
+            nc.scalar.activation(out=e[b, j][:], in_=sbank[b, j][:].rearrange("p j r -> p r j"), func=ACT.Exp,
+                                 bias=nbias[b, j][:], scale=SCALE, accum_out=tot[b, j][:])
+
+        def row_inv(b, j):
+            inv[b, j] = soft.tile([P, 1], F32, name="inv")
+            nc.vector.reciprocal(out=inv[b, j][:], in_=tot[b, j][:])
+
+        def row_out(b, j):
+            o = soft.tile([P, S], F32, name="o")
+            nc.vector.tensor_scalar(out=o[:], in0=e[b, j][:].rearrange("p r j -> p (r j)"), scalar1=inv[b, j][:], scalar2=None, op0=ALU.mult)
+            nc.sync.dma_start(out=out[b].rearrange("(r j) s -> r j s", j=J)[:, j, :], in_=o[:])
+
+        ctx.enter_context(tc.manual_schedule())
+        def dummy():
+            bank = psum.tile([P, 512], F32, name="bank", tag="bank")
+            nc.tensor.matmul(bank[:], lhsT=zero[:, 0:P], rhs=zero[:], start=True, stop=True)
+
+        def w_slots(m, f, *ss):
+            for s in ss:
+                w_slot(m, f, s)
+
+        for i in range(5):
+            dummy()
+        widen_v(0, 0)
+        widen_s(0, 1)
+        x_turn(0, 0)
+        w_slots(0, 0, 0)
+        dummy()
+        w_slots(0, 0, 1)
+        x_scale_out(0, 0)
+        x_turn(0, 1)
+        dummy()
+        x_quant(0, 0)
+        x_scale_out(0, 1)
+        widen_s(0, 2)
+        w_slots(0, 0, 2, 3)
+        dummy()
+        w_quant(0, 0, 0)
+        x_quant(0, 1)
+        widen_s(0, 3)
+        w_slots(0, 1, 0)
+        x_turn(0, 2)
+        dummy()
+        w_quant(0, 0, 1)
+        x_scale_out(0, 2)
+        w_slots(0, 1, 1, 2)
+        dummy()
+        w_slots(0, 1, 3)
+        x_turn(0, 3)
+        dummy()
+        x_scale_out(0, 3)
+        x_quant(0, 2)
+        x_quant(0, 3)
+        w_slots(1, 0, 0)
+        w_quant(0, 1, 0)
+        w_quant(0, 1, 1)
+        for j in range(J):
+            k_proj(0, 0, j)
+        widen_v(1, 0)
+        k_quant(0, 0, 0)
+        widen_v(1, 1)
+        k_quant(0, 0, 1)
+        w_slots(1, 0, 1, 2, 3)
+        x_turn(1, 0)
+        w_quant(1, 0, 0)
+        widen_v(1, 2)
+        w_quant(1, 0, 1)
+        widen_v(1, 3)
+        for j in range(J):
+            k_proj(0, 1, j)
+        k_quant(0, 1, 0)
+        x_scale_out(1, 0)
+        k_quant(0, 1, 1)
+        w_slots(1, 1, 0)
+        x_turn(1, 1)
+        x_scale_out(1, 1)
+        x_quant(1, 0)
+        x_quant(1, 1)
+        w_slots(1, 1, 1, 2, 3)
+        x_turn(1, 2)
+        x_turn(1, 3)
+        w_quant(1, 1, 0)
+        w_quant(1, 1, 1)
+        x_scale_out(1, 2)
+        x_scale_out(1, 3)
+        x_quant(1, 2)
+        x_quant(1, 3)
+        for f in range(F):
+            for j in range(J):
+                q_proj(0, f, j)
+        for j in range(J):
+            q_quant(0, j)
+        due = {}
+        for j in range(J):
+            due[j + 1] = (0, j)
+            due[j + 6] = (1, j)
+        for i in range(8):
+            j = i % 4
+            now, prev = due.get(i), due.get(i - 1)
+            proj = k_proj if i < 4 else q_proj
+            proj(1, 0, j)
+            if prev:
+                row_exp(*prev)
+            proj(1, 1, j, i in (1, 3, 5))
+            if i < 4 and i % 2:
+                k_quant(1, 0, i // 2)
+                k_quant(1, 1, i // 2)
+            if now:
+                scores(*now)
+            if prev:
+                row_inv(*prev)
+            if now:
+                row_bias(*now)
+            if i >= 4:
+                q_quant(1, j)
+            if prev:
+                row_out(*prev)
+        scores(1, 2)
+        scores(1, 3)
+        row_exp(1, 1)
+        row_bias(1, 2)
+        row_exp(1, 2)
+        row_inv(1, 1)
+        row_bias(1, 3)
+        row_exp(1, 3)
+        row_out(1, 1)
+        row_inv(1, 2)
+        row_out(1, 2)
+        row_inv(1, 3)
+        row_out(1, 3)

@@ -21,193 +21,161 @@ G = 2
 T = 4
 J = 4
 F = 2
+K, Q = 0, 1
 
 
 def tile_attentionnet_pa_kernel(tc, x_bytes, x_scale, wq, wk, out):
     nc = tc.nc
     with ExitStack() as ctx:
         keep = ctx.enter_context(tc.tile_pool(name="keep", bufs=1))
-        wgrp = ctx.enter_context(tc.tile_pool(name="wgrp", bufs=2))
-        stage = ctx.enter_context(tc.tile_pool(name="stage", bufs=3))
+        stage = ctx.enter_context(tc.tile_pool(name="stage", bufs=4))
         soft = ctx.enter_context(tc.tile_pool(name="soft", bufs=4))
         psum = ctx.enter_context(tc.psum_pool(name="psum", bufs=8))
 
-        xs = keep.tile([P, G, 2, 2], F32, name="xs")
-        xraw = [keep.tile([P, J, D], U8, name=f"xraw{b}") for b in range(B)]
-        wraw = {}
-        for m in range(2):
-            for f in range(F):
-                wraw[m, f] = keep.tile([P, T, D], BF16, name=f"wraw{m}{f}", align_bytes=64)
+        xs = keep.tile([P, G, T], F32, name="xs")
+        xraw, wraw = {}, {}
 
-        def load_x(b, js):
-            nc.sync.dma_start(out=xraw[b][:, js, :], in_=x_bytes[b].rearrange("(r j) k -> r j k", j=J)[:, js, :])
-
-        def load_xs():
-            nc.sync.dma_start(out=xs[:].rearrange("p g u e -> p g (u e)"), in_=x_scale.rearrange("o i (g p t) -> p (o i g) t", g=G, t=T))
+        def load_x(b, j0, n):
+            t = keep.tile([P, n, D], U8, name=f"xraw{b}{j0}")
+            nc.sync.dma_start(out=t[:], in_=x_bytes[b].rearrange("(r j) k -> r j k", j=J)[:, j0:j0 + n, :])
+            for i in range(n):
+                xraw[b, j0 + i] = t[:, i, :]
 
         def load_w(m, f, h):
+            t = keep.tile([P, 2, D], BF16, name=f"wraw{m}{f}{h}", align_bytes=64)
             rows = (wk, wq)[m][f * 512:(f + 1) * 512, :].rearrange("(m t) k -> m t k", t=T)
-            nc.sync.dma_start(out=wraw[m, f][:, 2 * h:2 * h + 2, :], in_=rows[:, 2 * h:2 * h + 2, :])
+            nc.sync.dma_start(out=t[:], in_=rows[:, 2 * h:2 * h + 2, :])
+            for i in range(2):
+                wraw[m, f, 2 * h + i] = t[:, i, :]
 
-        load_x(0, slice(0, 2))
-        load_xs()
-        load_w(0, 0, 0)
-        load_w(0, 0, 1)
-        load_x(0, slice(2, 4))
-        for m, f in ((0, 1), (1, 0)):
+        load_x(0, 0, 2)
+        nc.sync.dma_start(out=xs[:], in_=x_scale.rearrange("o i (g p t) -> p (o i g) t", g=G, t=T))
+        load_w(K, 0, 0)
+        load_w(K, 0, 1)
+        load_x(0, 2, 2)
+        for m, f in ((K, 1), (Q, 0)):
             for h in range(2):
                 load_w(m, f, h)
-        load_x(1, slice(0, 4))
+        load_x(1, 0, J)
         for h in range(2):
-            load_w(1, 1, h)
+            load_w(Q, 1, h)
 
         ident = keep.tile([P, P], F32, name="ident")
         make_identity(nc, ident[:])
-        warm = keep.tile([P, 1], F32, name="warm")
-        nc.vector.memset(warm[:], 0.0)
-        nc.scalar.activation(out=warm[:], in_=warm[:], func=ACT.Exp)
         zero = keep.tile([P, 512], BF16, name="zero")
         nc.vector.memset(zero[:], 0.0)
         one = keep.tile([P, 1], F32, name="one")
         nc.vector.memset(one[:], 1.0)
+        warm = keep.tile([P, 1], F32, name="warm")
+        nc.scalar.activation(out=warm[:], in_=one[:], func=ACT.Exp)
 
-        xw, xg = {}, {}
-        xc, xp = {}, {}
-        for b in range(B):
-            xc[b] = keep.tile([P, J, G, P], U32, name=f"xc{b}", align_bytes=64)
-            xp[b] = keep.tile([P, J, G, P], U8, name=f"xp{b}", align_bytes=64)
-        wc, wp = {}, {}
-        for m in range(2):
-            for f in range(F):
-                wc[m, f] = keep.tile([P, T, G, P], U32, name=f"wc{m}{f}", align_bytes=64)
-                wp[m, f] = keep.tile([P, T, G, P], U8, name=f"wp{m}{f}", align_bytes=64)
-        kc, kp = {}, {}
-        for b in range(B):
-            kc[b] = keep.tile([P, F, J, P], U32, name=f"kc{b}", align_bytes=64)
-            kp[b] = keep.tile([P, F, J, P], U8, name=f"kp{b}", align_bytes=64)
+        def mx_tiles(name, rows):
+            return (keep.tile([P, rows, P, T], BF16, name=name + "v", align_bytes=64),
+                    keep.tile([P, rows, P], U32, name=name + "c", align_bytes=64),
+                    keep.tile([P, rows, P], U8, name=name + "s", align_bytes=64))
 
-        def transposes(views):
-            bank = psum.tile([P, G, 2, P], F32, name="bank", tag="bank")
-            for g in range(G):
-                for u in range(2):
-                    nc.tensor.transpose(bank[:, g, u, :], views[g][u], ident[:])
-            return bank
+        xm = [mx_tiles(f"x{b}", J * G) for b in range(B)]
+        wm = {(m, f): mx_tiles(f"w{m}{f}", T * G) for m in (K, Q) for f in range(F)}
+        pm = {(m, b): mx_tiles(f"p{m}{b}", F * J) for m in (K, Q) for b in range(B)}
+
+        def quantize(tiles, first, n):
+            values, codes, scales = (t[:, first:first + n] for t in tiles)
+            nc.vector.quantize_mx(out=codes.rearrange("p a r -> p (a r)").bitcast(FP8X4),
+                                  scales=scales.rearrange("p a r -> p (a r)"),
+                                  in_=values.rearrange("p a r t -> p (a r t)"))
+
+        def operand(tiles, first, n=1):
+            return (tiles[1][:, first:first + n].rearrange("p a r -> p (a r)").bitcast(FP8X4),
+                    tiles[2][:, first:first + n].rearrange("p a r -> p (a r)"))
+
+        def new_bank():
+            return psum.tile([P, T, P], F32, name="bank")
+
+        def every_second(words, g, u):
+            return words[:, 256 * g + u:256 * (g + 1):2]
+
+        words, xbank = {}, {}
+        spread = keep.tile([P, G, P, T], F32, name="spread")
+
+        def spread_scales():
+            nc.vector.tensor_copy(out=spread[:], in_=xs[:].unsqueeze(2).to_broadcast([P, G, P, T]))
 
         def widen_v(b, j):
-            t = stage.tile([P, G, 2, P, 2], BF16, name="xwide", tag="xwide", bufs=4, align_bytes=64)
+            wide = stage.tile([P, 2, G * P, 2], BF16, name="wide", align_bytes=64)
+            nc.vector.tensor_scalar(out=wide[:].rearrange("r u c e -> r c u e"),
+                                    in0=xraw[b, j].bitcast(FP8).rearrange("r (c u e) -> r c u e", u=2, e=2),
+                                    scalar1=one[:], scalar2=None, op0=ALU.mult)
             for g in range(G):
-                nc.vector.tensor_scalar(out=t[:, g].rearrange("r u p e -> r p u e"),
-                                        in0=xraw[b][:, j, g * 512:(g + 1) * 512].bitcast(FP8).rearrange("r (p u e) -> r p u e", u=2, e=2),
-                                        scalar1=one[:], scalar2=None, op0=ALU.mult)
-            xw[b, j] = [[t[:, g, u].rearrange("r p e -> r (p e)").bitcast(F32) for u in range(2)] for g in range(G)]
-
-        def every_second(words):
-            return [[words[:, 256 * g + u:256 * (g + 1):2] for u in range(2)] for g in range(G)]
+                for u in range(2):
+                    words[b, j, g, u] = wide[:, u, g * P:(g + 1) * P].rearrange("r p e -> r (p e)").bitcast(F32)
 
         def widen_s(b, j):
-            t = stage.tile([P, D], BF16, name="xwide", tag="xwide", bufs=4, align_bytes=64)
-            nc.scalar.copy(out=t[:], in_=xraw[b][:, j, :].bitcast(FP8))
-            xw[b, j] = every_second(t[:].bitcast(F32))
-
-        xbank = {}
+            wide = stage.tile([P, D], BF16, name="wide", align_bytes=64)
+            nc.scalar.copy(out=wide[:], in_=xraw[b, j].bitcast(FP8))
+            for g in range(G):
+                for u in range(2):
+                    words[b, j, g, u] = every_second(wide[:].bitcast(F32), g, u)
 
         def x_turn(b, j):
-            xbank[b, j] = transposes(xw[b, j])
+            xbank[b, j] = new_bank()
+            for g in range(G):
+                for u in range(2):
+                    nc.tensor.transpose(xbank[b, j][:, G * u + g, :], words[b, j, g, u], ident[:])
 
         def x_scale_out(b, j):
-            bank = xbank[b, j]
-            grp = stage.tile([P, G, P, T], BF16, name="xgrp", tag="xgrp", bufs=4, align_bytes=64)
-            for g in range(G):
-                nc.vector.tensor_tensor(
-                    out=grp[:, g].rearrange("p r (u e) -> p r u e", u=2),
-                    in0=bank[:, g].bitcast(BF16).rearrange("p u (r e) -> p r u e", e=2),
-                    in1=xs[:, g].unsqueeze(1).to_broadcast([P, P, 2, 2]),
-                    op=ALU.mult)
-            xg[b, j] = grp
+            nc.vector.tensor_tensor(
+                out=xm[b][0][:, G * j:G * (j + 1)].rearrange("p g r (u e) -> p (g r) u e", u=2),
+                in0=xbank[b, j][:].bitcast(BF16).rearrange("p (u g) (r e) -> p (g r) u e", u=2, e=2),
+                in1=spread[:].rearrange("p g r (u e) -> p (g r) u e", u=2),
+                op=ALU.mult)
 
-        def x_quant(b, j):
-            grp = xg[b, j]
-            nc.vector.quantize_mx(
-                out=xc[b][:, j].rearrange("p g r -> p (g r)").bitcast(FP8X4),
-                scales=xp[b][:, j].rearrange("p g r -> p (g r)"),
-                in_=grp[:].rearrange("p g r t -> p (g r t)"))
+        def x_quant(b, j0, n=1):
+            quantize(xm[b], G * j0, G * n)
 
-        wg = {}
+        def w_slots(m, f, *slots):
+            for s in slots:
+                bank = new_bank()
+                for g in range(G):
+                    for u in range(2):
+                        nc.tensor.transpose(bank[:, 2 * g + u, :], every_second(wraw[m, f, s].bitcast(F32), g, u), ident[:])
+                nc.scalar.copy(out=wm[m, f][0][:, G * s:G * (s + 1)].bitcast(F32), in_=bank[:].rearrange("p (g u) r -> p g r u", u=2))
 
-        def w_slot(m, f, s):
-            if s == 0:
-                wg[m, f] = wgrp.tile([P, T, G, P, T], BF16, name="wgrp_t", tag="wgrp_t", align_bytes=64)
-            bank = transposes(every_second(wraw[m, f][:, s, :].bitcast(F32)))
-            nc.scalar.copy(out=wg[m, f][:, s].bitcast(F32), in_=bank[:].rearrange("p g u r -> p g r u"))
+        def w_quant(m, f, s0, n):
+            quantize(wm[m, f], G * s0, G * n)
 
-        def w_quant(m, f, h):
-                sl = slice(2 * h, 2 * h + 2)
-                nc.vector.quantize_mx(
-                    out=wc[m, f][:, sl].rearrange("p s g r -> p (s g r)").bitcast(FP8X4),
-                    scales=wp[m, f][:, sl].rearrange("p s g r -> p (s g r)"),
-                    in_=wg[m, f][:, sl].rearrange("p s g r t -> p (s g r t)"))
+        def row(m, f, j):
+            return J * f + j if m == K else F * j + f
 
-        def project(m, f, b, j, dst, vector):
-            bank = psum.tile([P, T, P], F32, name="bank", tag="bank")
+        def project(m, f, b, j, on_vector=False):
+            bank = new_bank()
             for t in range(T):
                 for g in range(G):
-                    nc.tensor.matmul_mx(
-                        out=bank[:, t, :],
-                        lhsT=wc[m, f][:, t, g, :].bitcast(FP8X4), lhsT_scale=wp[m, f][:, t, g, :],
-                        rhs=xc[b][:, j, g, :].bitcast(FP8X4), rhs_scale=xp[b][:, j, g, :],
-                        start=(g == 0), stop=(g == G - 1))
-            if vector:
+                    wc, ws = operand(wm[m, f], G * t + g)
+                    xc, xsc = operand(xm[b], G * j + g)
+                    nc.tensor.matmul_mx(out=bank[:, t, :], lhsT=wc, lhsT_scale=ws, rhs=xc, rhs_scale=xsc,
+                                        start=(g == 0), stop=(g == G - 1))
+            dst = pm[m, b][0][:, row(m, f, j)]
+            if on_vector:
                 nc.vector.tensor_copy(out=dst, in_=bank[:].rearrange("p t n -> p n t"))
             else:
                 nc.scalar.copy(out=dst, in_=bank[:].rearrange("p t n -> p n t"))
 
-        kg = {}
+        def p_quant(m, f, b, j, n):
+            quantize(pm[m, b], row(m, f, j), n)
 
-        def k_proj(b, f, j, vector=False):
-            if j % 2 == 0:
-                kg[b, f, j // 2] = stage.tile([P, 2, P, T], BF16, name="kgrp", tag="kgrp", bufs=4, align_bytes=64)
-            project(0, f, b, j, kg[b, f, j // 2][:, j % 2], vector)
-
-        def k_quant(b, f, h):
-            sl = slice(2 * h, 2 * h + 2)
-            nc.vector.quantize_mx(
-                out=kc[b][:, f, sl].rearrange("p j r -> p (j r)").bitcast(FP8X4),
-                scales=kp[b][:, f, sl].rearrange("p j r -> p (j r)"),
-                in_=kg[b, f, h][:].rearrange("p j r t -> p (j r t)"))
-
-        qc, qg = {}, {}
         sbank, nbias, e, tot, inv = {}, {}, {}, {}, {}
 
-        def q_proj(b, f, j, vector=False):
-            if (b, j) not in qg:
-                qg[b, j] = stage.tile([P, F, P, T], BF16, name="qgrp", tag="qgrp", bufs=5, align_bytes=64)
-            project(1, f, b, j, qg[b, j][:, f], vector)
-
-        def q_quant(b, j):
-            grp = qg[b, j]
-            c = stage.tile([P, F, P], U32, name="qcode", tag="qcode", bufs=6, align_bytes=64)
-            p = stage.tile([P, F, P], U8, name="qplane", tag="qplane", bufs=6, align_bytes=64)
-            nc.vector.quantize_mx(
-                out=c[:].rearrange("p f r -> p (f r)").bitcast(FP8X4),
-                scales=p[:].rearrange("p f r -> p (f r)"),
-                in_=grp[:].rearrange("p f r t -> p (f r t)"))
-            qc[b, j] = (c, p)
-
         def scores(b, j):
-            c, p = qc[b, j]
-            bank = psum.tile([P, J, P], F32, name="bank", tag="bank")
+            sbank[b, j] = new_bank()
             for f in range(F):
-                nc.tensor.matmul_mx(
-                    out=bank[:].rearrange("p j r -> p (j r)"),
-                    lhsT=c[:, f, :].bitcast(FP8X4), lhsT_scale=p[:, f, :],
-                    rhs=kc[b][:, f].rearrange("p j r -> p (j r)").bitcast(FP8X4),
-                    rhs_scale=kp[b][:, f].rearrange("p j r -> p (j r)"),
-                    start=(f == 0), stop=(f == F - 1))
-            sbank[b, j] = bank
+                qc, qs = operand(pm[Q, b], row(Q, f, j))
+                kc, ks = operand(pm[K, b], row(K, f, 0), J)
+                nc.tensor.matmul_mx(out=sbank[b, j][:].rearrange("p j r -> p (j r)"), lhsT=qc, lhsT_scale=qs, rhs=kc, rhs_scale=ks,
+                                    start=(f == 0), stop=(f == F - 1))
 
         def row_bias(b, j):
             nbias[b, j] = soft.tile([P, 1], F32, name="nbias")
-            scratch = soft.tile([P, S], F32, name="scratch")
+            scratch = soft.tile([P, S], F32, name="scratch", bufs=2)
             nc.vector.tensor_scalar(out=scratch[:], in0=sbank[b, j][:].rearrange("p j r -> p (j r)"), scalar1=-SCALE, scalar2=None,
                                     op0=ALU.mult, op1=ALU.min, accum_out=nbias[b, j][:])
 
@@ -221,126 +189,131 @@ def tile_attentionnet_pa_kernel(tc, x_bytes, x_scale, wq, wk, out):
             inv[b, j] = soft.tile([P, 1], F32, name="inv")
             nc.vector.reciprocal(out=inv[b, j][:], in_=tot[b, j][:])
 
-        def row_out(b, j):
+        def row_out(b, j, on_pool=False):
             o = soft.tile([P, S], F32, name="o")
-            nc.vector.tensor_scalar(out=o[:], in0=e[b, j][:].rearrange("p r j -> p (r j)"), scalar1=inv[b, j][:], scalar2=None, op0=ALU.mult)
+            if on_pool:
+                nc.gpsimd.tensor_scalar(out=o[:], in0=e[b, j][:].rearrange("p r j -> p (r j)"), scalar1=inv[b, j][:], scalar2=0.0, op0=ALU.mult, op1=ALU.add)
+            else:
+                nc.vector.tensor_scalar(out=o[:], in0=e[b, j][:].rearrange("p r j -> p (r j)"), scalar1=inv[b, j][:], scalar2=None, op0=ALU.mult)
             nc.sync.dma_start(out=out[b].rearrange("(r j) s -> r j s", j=J)[:, j, :], in_=o[:])
 
-        ctx.enter_context(tc.manual_schedule())
         def dummy():
-            bank = psum.tile([P, 512], F32, name="bank", tag="bank")
-            nc.tensor.matmul(bank[:], lhsT=zero[:, 0:P], rhs=zero[:], start=True, stop=True)
+            nc.tensor.matmul(new_bank()[:].rearrange("p t n -> p (t n)"), lhsT=zero[:, 0:P], rhs=zero[:], start=True, stop=True)
 
-        def w_slots(m, f, *ss):
-            for s in ss:
-                w_slot(m, f, s)
-
+        ctx.enter_context(tc.manual_schedule())
         for i in range(5):
             dummy()
         widen_v(0, 0)
+        spread_scales()
         widen_s(0, 1)
         x_turn(0, 0)
-        w_slots(0, 0, 0)
+        w_slots(K, 0, 0)
         dummy()
-        w_slots(0, 0, 1)
+        w_slots(K, 0, 1)
         x_scale_out(0, 0)
         x_turn(0, 1)
         dummy()
         x_quant(0, 0)
         x_scale_out(0, 1)
         widen_s(0, 2)
-        w_slots(0, 0, 2, 3)
+        w_slots(K, 0, 2, 3)
         dummy()
-        w_quant(0, 0, 0)
+        w_quant(K, 0, 0, 2)
         x_quant(0, 1)
         widen_s(0, 3)
-        w_slots(0, 1, 0)
+        w_slots(K, 1, 0)
         x_turn(0, 2)
         dummy()
-        w_quant(0, 0, 1)
+        w_quant(K, 0, 2, 2)
         x_scale_out(0, 2)
-        w_slots(0, 1, 1, 2)
+        w_slots(K, 1, 1, 2)
         dummy()
-        w_slots(0, 1, 3)
+        w_slots(K, 1, 3)
         x_turn(0, 3)
         dummy()
-        x_scale_out(0, 3)
         x_quant(0, 2)
+        x_scale_out(0, 3)
+        w_slots(Q, 0, 0)
+        for j in range(J - 1):
+            project(K, 0, 0, j)
         x_quant(0, 3)
-        w_slots(1, 0, 0)
-        w_quant(0, 1, 0)
-        w_quant(0, 1, 1)
-        for j in range(J):
-            k_proj(0, 0, j)
+        project(K, 0, 0, J - 1)
+        w_quant(K, 1, 0, T)
         widen_v(1, 0)
-        k_quant(0, 0, 0)
         widen_v(1, 1)
-        k_quant(0, 0, 1)
-        w_slots(1, 0, 1, 2, 3)
+        p_quant(K, 0, 0, 0, J)
+        w_slots(Q, 0, 1, 2, 3)
         x_turn(1, 0)
-        w_quant(1, 0, 0)
         widen_v(1, 2)
-        w_quant(1, 0, 1)
         widen_v(1, 3)
+        w_quant(Q, 0, 0, T)
         for j in range(J):
-            k_proj(0, 1, j)
-        k_quant(0, 1, 0)
+            project(K, 1, 0, j)
         x_scale_out(1, 0)
-        k_quant(0, 1, 1)
-        w_slots(1, 1, 0)
+        w_slots(Q, 1, 0)
         x_turn(1, 1)
+        p_quant(K, 1, 0, 0, J)
         x_scale_out(1, 1)
-        x_quant(1, 0)
-        x_quant(1, 1)
-        w_slots(1, 1, 1, 2, 3)
+        w_slots(Q, 1, 1, 2, 3)
         x_turn(1, 2)
         x_turn(1, 3)
-        w_quant(1, 1, 0)
-        w_quant(1, 1, 1)
+        w_quant(Q, 1, 0, 2)
+        x_quant(1, 0, 2)
+        w_quant(Q, 1, 2, 2)
         x_scale_out(1, 2)
         x_scale_out(1, 3)
-        x_quant(1, 2)
-        x_quant(1, 3)
         for f in range(F):
             for j in range(J):
-                q_proj(0, f, j)
-        for j in range(J):
-            q_quant(0, j)
-        due = {}
-        for j in range(J):
-            due[j + 1] = (0, j)
-            due[j + 6] = (1, j)
-        for i in range(8):
-            j = i % 4
-            now, prev = due.get(i), due.get(i - 1)
-            proj = k_proj if i < 4 else q_proj
-            proj(1, 0, j)
-            if prev:
-                row_exp(*prev)
-            proj(1, 1, j, i in (1, 3, 5))
-            if i < 4 and i % 2:
-                k_quant(1, 0, i // 2)
-                k_quant(1, 1, i // 2)
-            if now:
-                scores(*now)
-            if prev:
-                row_inv(*prev)
-            if now:
-                row_bias(*now)
-            if i >= 4:
-                q_quant(1, j)
-            if prev:
-                row_out(*prev)
+                project(Q, f, 0, j)
+        x_quant(1, 2, 2)
+        for j in range(0, J, 2):
+            p_quant(Q, 0, 0, j, 2 * F)
+        for i in range(6):
+            j = i % J
+            m = K if i < J else Q
+            project(m, 0, 1, j)
+            if i >= 2:
+                row_out(0, i - 2, False)
+            project(m, 1, 1, j, i in (1, 4))
+            if 1 <= i <= J:
+                row_exp(0, i - 1)
+            if i < J:
+                scores(0, i)
+            if i in (1, 3):
+                p_quant(K, 0, 1, i - 1, 2)
+            if i < J:
+                row_bias(0, i)
+            if i in (1, 3):
+                p_quant(K, 1, 1, i - 1, 2)
+            if i == 5:
+                p_quant(Q, 0, 1, 0, F)
+            if 1 <= i <= J:
+                row_inv(0, i - 1)
+        project(Q, 0, 1, 2)
+        p_quant(Q, 0, 1, 1, F)
+        project(Q, 0, 1, 3)
+        project(Q, 1, 1, 2, True)
+        scores(1, 0)
+        p_quant(Q, 0, 1, 3, 1)
+        row_bias(1, 0)
+        project(Q, 1, 1, 3)
+        p_quant(Q, 0, 1, 2, F)
+        row_exp(1, 0)
+        scores(1, 1)
+        row_bias(1, 1)
+        p_quant(Q, 1, 1, 3, 1)
         scores(1, 2)
         scores(1, 3)
         row_exp(1, 1)
+        row_inv(1, 0)
         row_bias(1, 2)
         row_exp(1, 2)
-        row_inv(1, 1)
+        row_out(1, 0)
         row_bias(1, 3)
         row_exp(1, 3)
-        row_out(1, 1)
+        row_inv(1, 1)
         row_inv(1, 2)
+        row_out(1, 1)
         row_out(1, 2)
         row_inv(1, 3)
         row_out(1, 3)

@@ -32,6 +32,8 @@ def tile_attentionnet_pa_kernel(tc, x_bytes, x_scale, wq, wk, out):
         soft = ctx.enter_context(tc.tile_pool(name="soft", bufs=4))
         psum = ctx.enter_context(tc.psum_pool(name="psum", bufs=8))
 
+        ctx.enter_context(tc.manual_schedule())
+
         xs = keep.tile([P, G, T], F32, name="xs")
         xraw, wraw = {}, {}
 
@@ -41,29 +43,32 @@ def tile_attentionnet_pa_kernel(tc, x_bytes, x_scale, wq, wk, out):
             for i in range(n):
                 xraw[b, j0 + i] = t[:, i, :]
 
-        def load_w(m, f, h):
-            t = keep.tile([P, 2, D], BF16, name=f"wraw{m}{f}{h}", align_bytes=64)
+        def load_w(m, f, s0, n):
+            t = keep.tile([P, n, D], BF16, name=f"wraw{m}{f}{s0}", align_bytes=64)
             rows = (wk, wq)[m][f * 512:(f + 1) * 512, :].rearrange("(m t) k -> m t k", t=T)
-            nc.sync.dma_start(out=t[:], in_=rows[:, 2 * h:2 * h + 2, :])
-            for i in range(2):
-                wraw[m, f, 2 * h + i] = t[:, i, :]
+            nc.sync.dma_start(out=t[:], in_=rows[:, s0:s0 + n, :])
+            for i in range(n):
+                wraw[m, f, s0 + i] = t[:, i, :]
 
-        load_x(0, 0, 2)
+        load_x(0, 0, 1)
         nc.sync.dma_start(out=xs[:], in_=x_scale.rearrange("o i (g p t) -> p (o i g) t", g=G, t=T))
-        load_w(K, 0, 0)
-        load_w(K, 0, 1)
+        load_x(0, 1, 1)
+        load_w(K, 0, 0, 1)
+        load_w(K, 0, 1, 1)
+        load_w(K, 0, 2, 2)
         load_x(0, 2, 2)
-        for m, f in ((K, 1), (Q, 0)):
-            for h in range(2):
-                load_w(m, f, h)
-        load_x(1, 0, J)
-        for h in range(2):
-            load_w(Q, 1, h)
+        load_w(K, 1, 0, 2)
+        load_w(K, 1, 2, 2)
+        load_w(Q, 0, 0, 2)
+        load_w(Q, 0, 2, 2)
+        load_x(1, 0, 4)
+        load_w(Q, 1, 0, 2)
+        load_w(Q, 1, 2, 2)
 
+        zero = keep.tile([P, 512], BF16, name="zero")
+        nc.gpsimd.memset(zero[:].bitcast(U32), 0)
         ident = keep.tile([P, P], F32, name="ident")
         make_identity(nc, ident[:])
-        zero = keep.tile([P, 512], BF16, name="zero")
-        nc.vector.memset(zero[:], 0.0)
         one = keep.tile([P, 1], F32, name="one")
         nc.vector.memset(one[:], 1.0)
         warm = keep.tile([P, 1], F32, name="warm")
@@ -88,17 +93,19 @@ def tile_attentionnet_pa_kernel(tc, x_bytes, x_scale, wq, wk, out):
             return (tiles[1][:, first:first + n].rearrange("p a r -> p (a r)").bitcast(FP8X4),
                     tiles[2][:, first:first + n].rearrange("p a r -> p (a r)"))
 
+        warm_ups = []
+
         def new_bank():
-            return psum.tile([P, T, P], F32, name="bank")
+            bank = psum.tile([P, T, P], F32, name="bank")
+            for n in warm_ups:
+                nc.tensor.matmul(bank[:].rearrange("p t n -> p (t n)"), lhsT=zero[:, 0:P], rhs=zero[:], start=True, stop=True)
+            warm_ups.clear()
+            return bank
 
         def every_second(words, g, u):
             return words[:, 256 * g + u:256 * (g + 1):2]
 
         words, xbank = {}, {}
-        spread = keep.tile([P, G, P, T], F32, name="spread")
-
-        def spread_scales():
-            nc.vector.tensor_copy(out=spread[:], in_=xs[:].unsqueeze(2).to_broadcast([P, G, P, T]))
 
         def widen_v(b, j):
             wide = stage.tile([P, 2, G * P, 2], BF16, name="wide", align_bytes=64)
@@ -123,21 +130,31 @@ def tile_attentionnet_pa_kernel(tc, x_bytes, x_scale, wq, wk, out):
                     nc.tensor.transpose(xbank[b, j][:, G * u + g, :], words[b, j, g, u], ident[:])
 
         def x_scale_out(b, j):
-            nc.vector.tensor_tensor(
-                out=xm[b][0][:, G * j:G * (j + 1)].rearrange("p g r (u e) -> p (g r) u e", u=2),
-                in0=xbank[b, j][:].bitcast(BF16).rearrange("p (u g) (r e) -> p (g r) u e", u=2, e=2),
-                in1=spread[:].rearrange("p g r (u e) -> p (g r) u e", u=2),
-                op=ALU.mult)
+            halves = xbank[b, j][:].bitcast(BF16).rearrange("p (u g) (r e) -> p g r u e", u=2, e=2)
+            for g in range(G):
+                nc.vector.tensor_tensor(
+                    out=xm[b][0][:, G * j + g].rearrange("p r (u e) -> p r u e", u=2),
+                    in0=halves[:, g],
+                    in1=xs[:, g].rearrange("p (u e) -> p u e", u=2).unsqueeze(1).to_broadcast([P, P, 2, 2]),
+                    op=ALU.mult)
 
         def x_quant(b, j0, n=1):
             quantize(xm[b], G * j0, G * n)
+
+        dealt = {}
+
+        def w_deal(m, f, *slots):
+            for s in slots:
+                dealt[m, f, s] = stage.tile([P, G, 2, P], F32, name="dealt", bufs=4, align_bytes=64)
+                nc.vector.tensor_copy(out=dealt[m, f, s][:], in_=wraw[m, f, s].bitcast(F32).rearrange("r (g p u) -> r g u p", g=G, u=2))
 
         def w_slots(m, f, *slots):
             for s in slots:
                 bank = new_bank()
                 for g in range(G):
                     for u in range(2):
-                        nc.tensor.transpose(bank[:, 2 * g + u, :], every_second(wraw[m, f, s].bitcast(F32), g, u), ident[:])
+                        view = dealt[m, f, s][:, g, u, :] if (m, f, s) in dealt else every_second(wraw[m, f, s].bitcast(F32), g, u)
+                        nc.tensor.transpose(bank[:, 2 * g + u, :], view, ident[:])
                 nc.scalar.copy(out=wm[m, f][0][:, G * s:G * (s + 1)].bitcast(F32), in_=bank[:].rearrange("p (g u) r -> p g r u", u=2))
 
         def w_quant(m, f, s0, n):
@@ -189,22 +206,20 @@ def tile_attentionnet_pa_kernel(tc, x_bytes, x_scale, wq, wk, out):
             inv[b, j] = soft.tile([P, 1], F32, name="inv")
             nc.vector.reciprocal(out=inv[b, j][:], in_=tot[b, j][:])
 
-        def row_out(b, j, on_pool=False):
-            o = soft.tile([P, S], F32, name="o")
-            if on_pool:
-                nc.gpsimd.tensor_scalar(out=o[:], in0=e[b, j][:].rearrange("p r j -> p (r j)"), scalar1=inv[b, j][:], scalar2=0.0, op0=ALU.mult, op1=ALU.add)
-            else:
-                nc.vector.tensor_scalar(out=o[:], in0=e[b, j][:].rearrange("p r j -> p (r j)"), scalar1=inv[b, j][:], scalar2=None, op0=ALU.mult)
-            nc.sync.dma_start(out=out[b].rearrange("(r j) s -> r j s", j=J)[:, j, :], in_=o[:])
+        def row_out(b, j, parts=1):
+            width = S // parts
+            for n in range(parts):
+                keys = slice(n * width, (n + 1) * width)
+                o = soft.tile([P, width], F32, name="o", bufs=5)
+                nc.vector.tensor_scalar(out=o[:], in0=e[b, j][:].rearrange("p r j -> p (r j)")[:, keys], scalar1=inv[b, j][:], scalar2=None, op0=ALU.mult)
+                nc.sync.dma_start(out=out[b].rearrange("(r j) s -> r j s", j=J)[:, j, keys], in_=o[:])
 
         def dummy():
-            nc.tensor.matmul(new_bank()[:].rearrange("p t n -> p (t n)"), lhsT=zero[:, 0:P], rhs=zero[:], start=True, stop=True)
+            warm_ups.append(1)
 
-        ctx.enter_context(tc.manual_schedule())
         for i in range(5):
             dummy()
         widen_v(0, 0)
-        spread_scales()
         widen_s(0, 1)
         x_turn(0, 0)
         w_slots(K, 0, 0)
@@ -230,50 +245,50 @@ def tile_attentionnet_pa_kernel(tc, x_bytes, x_scale, wq, wk, out):
         dummy()
         w_slots(K, 1, 3)
         x_turn(0, 3)
-        dummy()
         x_quant(0, 2)
         x_scale_out(0, 3)
-        w_slots(Q, 0, 0)
         for j in range(J - 1):
             project(K, 0, 0, j)
+        w_deal(Q, 0, 2, 3)
         x_quant(0, 3)
-        project(K, 0, 0, J - 1)
-        w_quant(K, 1, 0, T)
         widen_v(1, 0)
-        widen_v(1, 1)
-        p_quant(K, 0, 0, 0, J)
-        w_slots(Q, 0, 1, 2, 3)
+        w_quant(K, 1, 0, T)
+        w_slots(Q, 0, 0, 1, 2, 3)
         x_turn(1, 0)
-        widen_v(1, 2)
-        widen_v(1, 3)
+        widen_v(1, 1)
+        project(K, 0, 0, J - 1)
+        x_scale_out(1, 0)
         w_quant(Q, 0, 0, T)
         for j in range(J):
             project(K, 1, 0, j)
-        x_scale_out(1, 0)
+        widen_v(1, 2)
+        widen_v(1, 3)
         w_slots(Q, 1, 0)
         x_turn(1, 1)
-        p_quant(K, 1, 0, 0, J)
-        x_scale_out(1, 1)
         w_slots(Q, 1, 1, 2, 3)
+        x_scale_out(1, 1)
         x_turn(1, 2)
         x_turn(1, 3)
         w_quant(Q, 1, 0, 2)
-        x_quant(1, 0, 2)
-        w_quant(Q, 1, 2, 2)
         x_scale_out(1, 2)
+        w_quant(Q, 1, 2, 2)
         x_scale_out(1, 3)
+        x_quant(1, 0, 2)
+        for f in range(F):
+            p_quant(K, f, 0, 0, J)
         for f in range(F):
             for j in range(J):
                 project(Q, f, 0, j)
+                if (f, j) == (1, 1):
+                    p_quant(Q, 0, 0, 0, 2 * F)
         x_quant(1, 2, 2)
-        for j in range(0, J, 2):
-            p_quant(Q, 0, 0, j, 2 * F)
+        p_quant(Q, 0, 0, 2, 2 * F)
         for i in range(6):
             j = i % J
             m = K if i < J else Q
             project(m, 0, 1, j)
             if i >= 2:
-                row_out(0, i - 2, False)
+                row_out(0, i - 2)
             project(m, 1, 1, j, i in (1, 4))
             if 1 <= i <= J:
                 row_exp(0, i - 1)

@@ -55,8 +55,8 @@ def tile_attentionnet_pa_kernel(tc, x_bytes, x_scale, wq, wk, out):
         load_x(0, 1, 1)
         load_w(K, 0, 0, 1)
         load_w(K, 0, 1, 1)
-        load_w(K, 0, 2, 2)
         load_x(0, 2, 2)
+        load_w(K, 0, 2, 2)
         load_w(K, 1, 0, 2)
         load_w(K, 1, 2, 2)
         load_w(Q, 0, 0, 2)
@@ -93,14 +93,8 @@ def tile_attentionnet_pa_kernel(tc, x_bytes, x_scale, wq, wk, out):
             return (tiles[1][:, first:first + n].rearrange("p a r -> p (a r)").bitcast(FP8X4),
                     tiles[2][:, first:first + n].rearrange("p a r -> p (a r)"))
 
-        warm_ups = []
-
         def new_bank():
-            bank = psum.tile([P, T, P], F32, name="bank")
-            for n in warm_ups:
-                nc.tensor.matmul(bank[:].rearrange("p t n -> p (t n)"), lhsT=zero[:, 0:P], rhs=zero[:], start=True, stop=True)
-            warm_ups.clear()
-            return bank
+            return psum.tile([P, T, P], F32, name="bank")
 
         def every_second(words, g, u):
             return words[:, 256 * g + u:256 * (g + 1):2]
@@ -215,7 +209,7 @@ def tile_attentionnet_pa_kernel(tc, x_bytes, x_scale, wq, wk, out):
                 nc.sync.dma_start(out=out[b].rearrange("(r j) s -> r j s", j=J)[:, j, keys], in_=o[:])
 
         def dummy():
-            warm_ups.append(1)
+            nc.tensor.matmul(new_bank()[:].rearrange("p t n -> p (t n)"), lhsT=zero[:, 0:P], rhs=zero[:], start=True, stop=True)
 
         for i in range(5):
             dummy()
@@ -223,49 +217,47 @@ def tile_attentionnet_pa_kernel(tc, x_bytes, x_scale, wq, wk, out):
         widen_s(0, 1)
         x_turn(0, 0)
         w_slots(K, 0, 0)
+        x_scale_out(0, 0)
         dummy()
         w_slots(K, 0, 1)
-        x_scale_out(0, 0)
         x_turn(0, 1)
-        dummy()
+        widen_v(0, 2)
+        widen_s(0, 3)
         x_quant(0, 0)
         x_scale_out(0, 1)
-        widen_s(0, 2)
-        w_slots(K, 0, 2, 3)
         dummy()
+        x_turn(0, 2)
         w_quant(K, 0, 0, 2)
         x_quant(0, 1)
-        widen_s(0, 3)
-        w_slots(K, 1, 0)
-        x_turn(0, 2)
-        dummy()
-        w_quant(K, 0, 2, 2)
         x_scale_out(0, 2)
-        w_slots(K, 1, 1, 2)
         dummy()
-        w_slots(K, 1, 3)
+        w_slots(K, 0, 2, 3)
+        dummy()
         x_turn(0, 3)
         x_quant(0, 2)
+        w_slots(K, 1, 0, 1)
+        w_quant(K, 0, 2, 2)
         x_scale_out(0, 3)
-        for j in range(J - 1):
-            project(K, 0, 0, j)
-        w_deal(Q, 0, 2, 3)
+        dummy()
+        w_slots(K, 1, 2, 3)
         x_quant(0, 3)
-        widen_v(1, 0)
+        for j in range(J):
+            project(K, 0, 0, j)
+        w_deal(Q, 0, 0, 1)
         w_quant(K, 1, 0, T)
         w_slots(Q, 0, 0, 1, 2, 3)
-        x_turn(1, 0)
+        p_quant(K, 0, 0, 0, J)
+        widen_v(1, 0)
         widen_v(1, 1)
-        project(K, 0, 0, J - 1)
-        x_scale_out(1, 0)
-        w_quant(Q, 0, 0, T)
         for j in range(J):
             project(K, 1, 0, j)
+        w_quant(Q, 0, 0, T)
         widen_v(1, 2)
-        widen_v(1, 3)
-        w_slots(Q, 1, 0)
+        x_turn(1, 0)
         x_turn(1, 1)
-        w_slots(Q, 1, 1, 2, 3)
+        widen_v(1, 3)
+        x_scale_out(1, 0)
+        w_slots(Q, 1, 0, 1, 2, 3)
         x_scale_out(1, 1)
         x_turn(1, 2)
         x_turn(1, 3)
@@ -274,8 +266,7 @@ def tile_attentionnet_pa_kernel(tc, x_bytes, x_scale, wq, wk, out):
         w_quant(Q, 1, 2, 2)
         x_scale_out(1, 3)
         x_quant(1, 0, 2)
-        for f in range(F):
-            p_quant(K, f, 0, 0, J)
+        p_quant(K, 1, 0, 0, J)
         for f in range(F):
             for j in range(J):
                 project(Q, f, 0, j)
@@ -307,28 +298,28 @@ def tile_attentionnet_pa_kernel(tc, x_bytes, x_scale, wq, wk, out):
         project(Q, 0, 1, 2)
         p_quant(Q, 0, 1, 1, F)
         project(Q, 0, 1, 3)
-        project(Q, 1, 1, 2, True)
         scores(1, 0)
-        p_quant(Q, 0, 1, 3, 1)
         row_bias(1, 0)
-        project(Q, 1, 1, 3)
-        p_quant(Q, 0, 1, 2, F)
+        project(Q, 1, 1, 2, True)
         row_exp(1, 0)
+        project(Q, 1, 1, 3)
+        p_quant(Q, 0, 1, 3, 1)
+        p_quant(Q, 0, 1, 2, F)
+        row_inv(1, 0)
         scores(1, 1)
         row_bias(1, 1)
         p_quant(Q, 1, 1, 3, 1)
         scores(1, 2)
         scores(1, 3)
         row_exp(1, 1)
-        row_inv(1, 0)
+        row_out(1, 0)
         row_bias(1, 2)
         row_exp(1, 2)
-        row_out(1, 0)
+        row_inv(1, 1)
         row_bias(1, 3)
         row_exp(1, 3)
-        row_inv(1, 1)
-        row_inv(1, 2)
         row_out(1, 1)
+        row_inv(1, 2)
         row_out(1, 2)
         row_inv(1, 3)
         row_out(1, 3)

@@ -22,6 +22,9 @@ T = 4
 J = 4
 F = 2
 K, Q = 0, 1
+BANK = 512
+FIRST_WARM_UP = 320
+VECTOR_COPIES = (1, 4)
 
 
 def tile_attentionnet_pa_kernel(tc, x_bytes, x_scale, wq, wk, out):
@@ -31,42 +34,40 @@ def tile_attentionnet_pa_kernel(tc, x_bytes, x_scale, wq, wk, out):
         stage = ctx.enter_context(tc.tile_pool(name="stage", bufs=4))
         soft = ctx.enter_context(tc.tile_pool(name="soft", bufs=4))
         psum = ctx.enter_context(tc.psum_pool(name="psum", bufs=8))
-
         ctx.enter_context(tc.manual_schedule())
 
         xs = keep.tile([P, G, T], F32, name="xs")
         xraw, wraw = {}, {}
 
         def load_x(b, j0, n):
-            t = keep.tile([P, n, D], U8, name=f"xraw{b}{j0}")
-            nc.sync.dma_start(out=t[:], in_=x_bytes[b].rearrange("(r j) k -> r j k", j=J)[:, j0:j0 + n, :])
+            raw = keep.tile([P, n, D], U8, name=f"xraw{b}{j0}")
+            nc.sync.dma_start(out=raw[:], in_=x_bytes[b].rearrange("(r j) k -> r j k", j=J)[:, j0:j0 + n, :])
             for i in range(n):
-                xraw[b, j0 + i] = t[:, i, :]
+                xraw[b, j0 + i] = raw[:, i, :]
 
         def load_w(m, f, s0, n):
-            t = keep.tile([P, n, D], BF16, name=f"wraw{m}{f}{s0}", align_bytes=64)
+            raw = keep.tile([P, n, D], BF16, name=f"wraw{m}{f}{s0}", align_bytes=64)
             rows = (wk, wq)[m][f * 512:(f + 1) * 512, :].rearrange("(m t) k -> m t k", t=T)
-            nc.sync.dma_start(out=t[:], in_=rows[:, s0:s0 + n, :])
+            nc.sync.dma_start(out=raw[:], in_=rows[:, s0:s0 + n, :])
             for i in range(n):
-                wraw[m, f, s0 + i] = t[:, i, :]
+                wraw[m, f, s0 + i] = raw[:, i, :]
 
         load_x(0, 0, 1)
         nc.sync.dma_start(out=xs[:], in_=x_scale.rearrange("o i (g p t) -> p (o i g) t", g=G, t=T))
         load_x(0, 1, 1)
+        load_x(0, 2, 2)
         load_w(K, 0, 0, 1)
         load_w(K, 0, 1, 1)
-        load_x(0, 2, 2)
         load_w(K, 0, 2, 2)
-        load_w(K, 1, 0, 2)
-        load_w(K, 1, 2, 2)
-        load_w(Q, 0, 0, 2)
-        load_w(Q, 0, 2, 2)
-        load_x(1, 0, 4)
-        load_w(Q, 1, 0, 2)
-        load_w(Q, 1, 2, 2)
+        for m, f in ((K, 1), (Q, 0)):
+            for s0 in (0, 2):
+                load_w(m, f, s0, 2)
+        load_x(1, 0, J)
+        for s0 in (0, 2):
+            load_w(Q, 1, s0, 2)
 
-        zero = keep.tile([P, 512], BF16, name="zero")
-        nc.gpsimd.memset(zero[:].bitcast(U32), 0)
+        zero = keep.tile([P, FIRST_WARM_UP], F32, name="zero")
+        nc.gpsimd.memset(zero[:], 0.0)
         ident = keep.tile([P, P], F32, name="ident")
         make_identity(nc, ident[:])
         one = keep.tile([P, 1], F32, name="one")
@@ -83,8 +84,11 @@ def tile_attentionnet_pa_kernel(tc, x_bytes, x_scale, wq, wk, out):
         wm = {(m, f): mx_tiles(f"w{m}{f}", T * G) for m in (K, Q) for f in range(F)}
         pm = {(m, b): mx_tiles(f"p{m}{b}", F * J) for m in (K, Q) for b in range(B)}
 
+        def p_row(m, f, j):
+            return J * f + j if m == K else F * j + f
+
         def quantize(tiles, first, n):
-            values, codes, scales = (t[:, first:first + n] for t in tiles)
+            values, codes, scales = (tile[:, first:first + n] for tile in tiles)
             nc.vector.quantize_mx(out=codes.rearrange("p a r -> p (a r)").bitcast(FP8X4),
                                   scales=scales.rearrange("p a r -> p (a r)"),
                                   in_=values.rearrange("p a r t -> p (a r t)"))
@@ -96,32 +100,41 @@ def tile_attentionnet_pa_kernel(tc, x_bytes, x_scale, wq, wk, out):
         def new_bank():
             return psum.tile([P, T, P], F32, name="bank")
 
-        def every_second(words, g, u):
-            return words[:, 256 * g + u:256 * (g + 1):2]
+        def every_second(pairs, g, u):
+            return pairs[:, 256 * g + u:256 * (g + 1):2]
 
-        words, xbank = {}, {}
+        def first_warm_up():
+            nc.tensor.matmul(new_bank()[:].rearrange("p t n -> p (t n)")[:, 0:FIRST_WARM_UP],
+                             lhsT=zero[:, 0:P], rhs=zero[:], start=True, stop=True)
 
-        def widen_v(b, j):
+        def warm_up():
+            zero16 = zero[:].bitcast(BF16)
+            nc.tensor.matmul(new_bank()[:].rearrange("p t n -> p (t n)"),
+                             lhsT=zero16[:, 0:P], rhs=zero16[:, 0:BANK], start=True, stop=True)
+
+        xwords, xbank = {}, {}
+
+        def widen_on_vector(b, j):
             wide = stage.tile([P, 2, G * P, 2], BF16, name="wide", align_bytes=64)
             nc.vector.tensor_scalar(out=wide[:].rearrange("r u c e -> r c u e"),
                                     in0=xraw[b, j].bitcast(FP8).rearrange("r (c u e) -> r c u e", u=2, e=2),
                                     scalar1=one[:], scalar2=None, op0=ALU.mult)
             for g in range(G):
                 for u in range(2):
-                    words[b, j, g, u] = wide[:, u, g * P:(g + 1) * P].rearrange("r p e -> r (p e)").bitcast(F32)
+                    xwords[b, j, g, u] = wide[:, u, g * P:(g + 1) * P].rearrange("r p e -> r (p e)").bitcast(F32)
 
-        def widen_s(b, j):
+        def widen_on_scalar(b, j):
             wide = stage.tile([P, D], BF16, name="wide", align_bytes=64)
             nc.scalar.copy(out=wide[:], in_=xraw[b, j].bitcast(FP8))
             for g in range(G):
                 for u in range(2):
-                    words[b, j, g, u] = every_second(wide[:].bitcast(F32), g, u)
+                    xwords[b, j, g, u] = every_second(wide[:].bitcast(F32), g, u)
 
         def x_turn(b, j):
             xbank[b, j] = new_bank()
             for g in range(G):
                 for u in range(2):
-                    nc.tensor.transpose(xbank[b, j][:, G * u + g, :], words[b, j, g, u], ident[:])
+                    nc.tensor.transpose(xbank[b, j][:, G * u + g, :], xwords[b, j, g, u], ident[:])
 
         def x_scale_out(b, j):
             halves = xbank[b, j][:].bitcast(BF16).rearrange("p (u g) (r e) -> p g r u e", u=2, e=2)
@@ -132,63 +145,64 @@ def tile_attentionnet_pa_kernel(tc, x_bytes, x_scale, wq, wk, out):
                     in1=xs[:, g].rearrange("p (u e) -> p u e", u=2).unsqueeze(1).to_broadcast([P, P, 2, 2]),
                     op=ALU.mult)
 
-        def x_quant(b, j0, n=1):
+        def x_quant(b, j0, n):
             quantize(xm[b], G * j0, G * n)
 
         dealt = {}
 
-        def w_deal(m, f, *slots):
-            for s in slots:
-                dealt[m, f, s] = stage.tile([P, G, 2, P], F32, name="dealt", bufs=4, align_bytes=64)
-                nc.vector.tensor_copy(out=dealt[m, f, s][:], in_=wraw[m, f, s].bitcast(F32).rearrange("r (g p u) -> r g u p", g=G, u=2))
+        def w_deal(m, f, s):
+            dealt[m, f, s] = stage.tile([P, G, 2, P], F32, name="dealt", align_bytes=64)
+            nc.vector.tensor_copy(out=dealt[m, f, s][:],
+                                  in_=wraw[m, f, s].bitcast(F32).rearrange("r (g p u) -> r g u p", g=G, u=2))
 
-        def w_slots(m, f, *slots):
+        def w_turn(m, f, *slots):
             for s in slots:
                 bank = new_bank()
                 for g in range(G):
                     for u in range(2):
-                        view = dealt[m, f, s][:, g, u, :] if (m, f, s) in dealt else every_second(wraw[m, f, s].bitcast(F32), g, u)
+                        if (m, f, s) in dealt:
+                            view = dealt[m, f, s][:, g, u, :]
+                        else:
+                            view = every_second(wraw[m, f, s].bitcast(F32), g, u)
                         nc.tensor.transpose(bank[:, 2 * g + u, :], view, ident[:])
-                nc.scalar.copy(out=wm[m, f][0][:, G * s:G * (s + 1)].bitcast(F32), in_=bank[:].rearrange("p (g u) r -> p g r u", u=2))
+                nc.scalar.copy(out=wm[m, f][0][:, G * s:G * (s + 1)].bitcast(F32),
+                               in_=bank[:].rearrange("p (g u) r -> p g r u", u=2))
 
         def w_quant(m, f, s0, n):
             quantize(wm[m, f], G * s0, G * n)
 
-        def row(m, f, j):
-            return J * f + j if m == K else F * j + f
-
         def project(m, f, b, j, on_vector=False):
             bank = new_bank()
-            for t in range(T):
+            for s in range(T):
                 for g in range(G):
-                    wc, ws = operand(wm[m, f], G * t + g)
+                    wc, wsc = operand(wm[m, f], G * s + g)
                     xc, xsc = operand(xm[b], G * j + g)
-                    nc.tensor.matmul_mx(out=bank[:, t, :], lhsT=wc, lhsT_scale=ws, rhs=xc, rhs_scale=xsc,
+                    nc.tensor.matmul_mx(out=bank[:, s, :], lhsT=wc, lhsT_scale=wsc, rhs=xc, rhs_scale=xsc,
                                         start=(g == 0), stop=(g == G - 1))
-            dst = pm[m, b][0][:, row(m, f, j)]
+            dst = pm[m, b][0][:, p_row(m, f, j)]
             if on_vector:
                 nc.vector.tensor_copy(out=dst, in_=bank[:].rearrange("p t n -> p n t"))
             else:
                 nc.scalar.copy(out=dst, in_=bank[:].rearrange("p t n -> p n t"))
 
         def p_quant(m, f, b, j, n):
-            quantize(pm[m, b], row(m, f, j), n)
+            quantize(pm[m, b], p_row(m, f, j), n)
 
         sbank, nbias, e, tot, inv = {}, {}, {}, {}, {}
 
         def scores(b, j):
             sbank[b, j] = new_bank()
             for f in range(F):
-                qc, qs = operand(pm[Q, b], row(Q, f, j))
-                kc, ks = operand(pm[K, b], row(K, f, 0), J)
-                nc.tensor.matmul_mx(out=sbank[b, j][:].rearrange("p j r -> p (j r)"), lhsT=qc, lhsT_scale=qs, rhs=kc, rhs_scale=ks,
-                                    start=(f == 0), stop=(f == F - 1))
+                qc, qsc = operand(pm[Q, b], p_row(Q, f, j))
+                kc, ksc = operand(pm[K, b], p_row(K, f, 0), J)
+                nc.tensor.matmul_mx(out=sbank[b, j][:].rearrange("p j r -> p (j r)"), lhsT=qc, lhsT_scale=qsc,
+                                    rhs=kc, rhs_scale=ksc, start=(f == 0), stop=(f == F - 1))
 
         def row_bias(b, j):
             nbias[b, j] = soft.tile([P, 1], F32, name="nbias")
-            scratch = soft.tile([P, S], F32, name="scratch", bufs=2)
-            nc.vector.tensor_scalar(out=scratch[:], in0=sbank[b, j][:].rearrange("p j r -> p (j r)"), scalar1=-SCALE, scalar2=None,
-                                    op0=ALU.mult, op1=ALU.min, accum_out=nbias[b, j][:])
+            scaled = soft.tile([P, S], F32, name="scaled", bufs=2)
+            nc.vector.tensor_scalar(out=scaled[:], in0=sbank[b, j][:].rearrange("p j r -> p (j r)"), scalar1=-SCALE,
+                                    scalar2=None, op0=ALU.mult, op1=ALU.min, accum_out=nbias[b, j][:])
 
         def row_exp(b, j):
             e[b, j] = soft.tile([P, P, J], F32, name="e")
@@ -200,71 +214,64 @@ def tile_attentionnet_pa_kernel(tc, x_bytes, x_scale, wq, wk, out):
             inv[b, j] = soft.tile([P, 1], F32, name="inv")
             nc.vector.reciprocal(out=inv[b, j][:], in_=tot[b, j][:])
 
-        def row_out(b, j, parts=1):
-            width = S // parts
-            for n in range(parts):
-                keys = slice(n * width, (n + 1) * width)
-                o = soft.tile([P, width], F32, name="o", bufs=5)
-                nc.vector.tensor_scalar(out=o[:], in0=e[b, j][:].rearrange("p r j -> p (r j)")[:, keys], scalar1=inv[b, j][:], scalar2=None, op0=ALU.mult)
-                nc.sync.dma_start(out=out[b].rearrange("(r j) s -> r j s", j=J)[:, j, keys], in_=o[:])
+        def row_out(b, j):
+            prob = soft.tile([P, S], F32, name="prob", bufs=5)
+            nc.vector.tensor_scalar(out=prob[:], in0=e[b, j][:].rearrange("p r j -> p (r j)"), scalar1=inv[b, j][:],
+                                    scalar2=None, op0=ALU.mult)
+            nc.sync.dma_start(out=out[b].rearrange("(r j) s -> r j s", j=J)[:, j, :], in_=prob[:])
 
-        def dummy():
-            nc.tensor.matmul(new_bank()[:].rearrange("p t n -> p (t n)"), lhsT=zero[:, 0:P], rhs=zero[:], start=True, stop=True)
-
-        for i in range(5):
-            dummy()
-        widen_v(0, 0)
-        widen_s(0, 1)
+        first_warm_up()
+        first_warm_up()
+        widen_on_vector(0, 0)
+        widen_on_scalar(0, 1)
         x_turn(0, 0)
-        w_slots(K, 0, 0)
+        widen_on_vector(0, 2)
+        widen_on_scalar(0, 3)
         x_scale_out(0, 0)
-        dummy()
-        w_slots(K, 0, 1)
-        x_turn(0, 1)
-        widen_v(0, 2)
-        widen_s(0, 3)
-        x_quant(0, 0)
+        warm_up()
+        for j in (1, 2):
+            x_turn(0, j)
         x_scale_out(0, 1)
-        dummy()
-        x_turn(0, 2)
-        w_quant(K, 0, 0, 2)
-        x_quant(0, 1)
-        x_scale_out(0, 2)
-        dummy()
-        w_slots(K, 0, 2, 3)
-        dummy()
+        x_quant(0, 0, 1)
+        warm_up()
+        w_turn(K, 0, 0)
         x_turn(0, 3)
-        x_quant(0, 2)
-        w_slots(K, 1, 0, 1)
-        w_quant(K, 0, 2, 2)
+        x_scale_out(0, 2)
+        x_quant(0, 1, 1)
         x_scale_out(0, 3)
-        dummy()
-        w_slots(K, 1, 2, 3)
-        x_quant(0, 3)
+        warm_up()
+        w_turn(K, 0, 1, 2, 3)
+        for s0 in (0, 2):
+            w_quant(K, 0, s0, 2)
+        x_quant(0, 2, 2)
+        for s0 in (0, 2):
+            warm_up()
+            w_turn(K, 1, s0, s0 + 1)
+
         for j in range(J):
             project(K, 0, 0, j)
-        w_deal(Q, 0, 0, 1)
+        for s in (0, 1):
+            w_deal(Q, 0, s)
         w_quant(K, 1, 0, T)
-        w_slots(Q, 0, 0, 1, 2, 3)
+        w_turn(Q, 0, 0, 1, 2, 3)
         p_quant(K, 0, 0, 0, J)
-        widen_v(1, 0)
-        widen_v(1, 1)
+        for j in (0, 1):
+            widen_on_vector(1, j)
         for j in range(J):
             project(K, 1, 0, j)
         w_quant(Q, 0, 0, T)
-        widen_v(1, 2)
-        x_turn(1, 0)
-        x_turn(1, 1)
-        widen_v(1, 3)
+        widen_on_vector(1, 2)
+        for j in (0, 1):
+            x_turn(1, j)
+        widen_on_vector(1, 3)
         x_scale_out(1, 0)
-        w_slots(Q, 1, 0, 1, 2, 3)
+        w_turn(Q, 1, 0, 1, 2, 3)
         x_scale_out(1, 1)
-        x_turn(1, 2)
-        x_turn(1, 3)
-        w_quant(Q, 1, 0, 2)
-        x_scale_out(1, 2)
-        w_quant(Q, 1, 2, 2)
-        x_scale_out(1, 3)
+        for j in (2, 3):
+            x_turn(1, j)
+        w_quant(Q, 1, 0, T)
+        for j in (2, 3):
+            x_scale_out(1, j)
         x_quant(1, 0, 2)
         p_quant(K, 1, 0, 0, J)
         for f in range(F):
@@ -274,27 +281,29 @@ def tile_attentionnet_pa_kernel(tc, x_bytes, x_scale, wq, wk, out):
                     p_quant(Q, 0, 0, 0, 2 * F)
         x_quant(1, 2, 2)
         p_quant(Q, 0, 0, 2, 2 * F)
-        for i in range(6):
-            j = i % J
-            m = K if i < J else Q
+
+        for i in range(J + 2):
+            m, j = (K, i) if i < J else (Q, i - J)
             project(m, 0, 1, j)
+            if i == J + 1:
+                p_quant(Q, 0, 1, 0, F)
             if i >= 2:
                 row_out(0, i - 2)
-            project(m, 1, 1, j, i in (1, 4))
+            project(m, 1, 1, j, i in VECTOR_COPIES)
             if 1 <= i <= J:
                 row_exp(0, i - 1)
+            pair_done = i < J and i % 2 == 1
             if i < J:
                 scores(0, i)
-            if i in (1, 3):
+            if pair_done:
                 p_quant(K, 0, 1, i - 1, 2)
             if i < J:
                 row_bias(0, i)
-            if i in (1, 3):
+            if pair_done:
                 p_quant(K, 1, 1, i - 1, 2)
-            if i == 5:
-                p_quant(Q, 0, 1, 0, F)
             if 1 <= i <= J:
                 row_inv(0, i - 1)
+
         project(Q, 0, 1, 2)
         p_quant(Q, 0, 1, 1, F)
         project(Q, 0, 1, 3)
@@ -313,13 +322,12 @@ def tile_attentionnet_pa_kernel(tc, x_bytes, x_scale, wq, wk, out):
         scores(1, 3)
         row_exp(1, 1)
         row_out(1, 0)
-        row_bias(1, 2)
-        row_exp(1, 2)
-        row_inv(1, 1)
-        row_bias(1, 3)
-        row_exp(1, 3)
+        for j in (2, 3):
+            row_bias(1, j)
+            row_exp(1, j)
+            if j == 2:
+                row_inv(1, 1)
         row_out(1, 1)
-        row_inv(1, 2)
-        row_out(1, 2)
-        row_inv(1, 3)
-        row_out(1, 3)
+        for j in (2, 3):
+            row_inv(1, j)
+            row_out(1, j)

@@ -24,7 +24,7 @@ F = 2
 K, Q = 0, 1
 BANK = 512
 FIRST_WARM_UP = 320
-VECTOR_COPIES = (1, 4)
+VECTOR_COPY = 1
 
 
 def tile_attentionnet_pa_kernel(tc, x_bytes, x_scale, wq, wk, out):
@@ -134,16 +134,14 @@ def tile_attentionnet_pa_kernel(tc, x_bytes, x_scale, wq, wk, out):
             xbank[b, j] = new_bank()
             for g in range(G):
                 for u in range(2):
-                    nc.tensor.transpose(xbank[b, j][:, G * u + g, :], xwords[b, j, g, u], ident[:])
+                    nc.tensor.transpose(xbank[b, j][:, 2 * g + u, :], xwords[b, j, g, u], ident[:])
 
         def x_scale_out(b, j):
-            halves = xbank[b, j][:].bitcast(BF16).rearrange("p (u g) (r e) -> p g r u e", u=2, e=2)
-            for g in range(G):
-                nc.vector.tensor_tensor(
-                    out=xm[b][0][:, G * j + g].rearrange("p r (u e) -> p r u e", u=2),
-                    in0=halves[:, g],
-                    in1=xs[:, g].rearrange("p (u e) -> p u e", u=2).unsqueeze(1).to_broadcast([P, P, 2, 2]),
-                    op=ALU.mult)
+            nc.vector.tensor_tensor(
+                out=xm[b][0][:, G * j:G * (j + 1)].rearrange("p g r (u e) -> p r g u e", u=2),
+                in0=xbank[b, j][:].bitcast(BF16).rearrange("p (g u) (r e) -> p r g u e", u=2, e=2),
+                in1=xs[:].rearrange("p g (u e) -> p g u e", u=2).unsqueeze(1).to_broadcast([P, P, G, 2, 2]),
+                op=ALU.mult)
 
         def x_quant(b, j0, n):
             quantize(xm[b], G * j0, G * n)
@@ -222,50 +220,51 @@ def tile_attentionnet_pa_kernel(tc, x_bytes, x_scale, wq, wk, out):
 
         first_warm_up()
         first_warm_up()
-        widen_on_vector(0, 0)
-        widen_on_scalar(0, 1)
-        x_turn(0, 0)
-        widen_on_vector(0, 2)
-        widen_on_scalar(0, 3)
-        x_scale_out(0, 0)
-        warm_up()
-        for j in (1, 2):
+        for j in (0, 1):
+            widen_on_vector(0, j)
+        for j in (2, 3):
+            widen_on_scalar(0, j)
+        for j in (0, 1):
             x_turn(0, j)
-        x_scale_out(0, 1)
-        x_quant(0, 0, 1)
+            x_scale_out(0, j)
         warm_up()
         w_turn(K, 0, 0)
-        x_turn(0, 3)
+        x_turn(0, 2)
         x_scale_out(0, 2)
-        x_quant(0, 1, 1)
+        x_quant(0, 0, 2)
+        w_turn(K, 0, 1)
+        x_turn(0, 3)
         x_scale_out(0, 3)
         warm_up()
-        w_turn(K, 0, 1, 2, 3)
+        w_turn(K, 0, 2, 3)
         for s0 in (0, 2):
             w_quant(K, 0, s0, 2)
         x_quant(0, 2, 2)
         for s0 in (0, 2):
             warm_up()
             w_turn(K, 1, s0, s0 + 1)
-
         for j in range(J):
             project(K, 0, 0, j)
         for s in (0, 1):
             w_deal(Q, 0, s)
         w_quant(K, 1, 0, T)
+        for s in (2, 3):
+            w_deal(Q, 0, s)
         w_turn(Q, 0, 0, 1, 2, 3)
-        p_quant(K, 0, 0, 0, J)
         for j in (0, 1):
             widen_on_vector(1, j)
+        p_quant(K, 0, 0, 0, J)
         for j in range(J):
             project(K, 1, 0, j)
-        w_quant(Q, 0, 0, T)
         widen_on_vector(1, 2)
+        w_quant(Q, 0, 0, T)
         for j in (0, 1):
             x_turn(1, j)
         widen_on_vector(1, 3)
         x_scale_out(1, 0)
-        w_turn(Q, 1, 0, 1, 2, 3)
+        w_turn(Q, 1, 0, 1)
+        warm_up()
+        w_turn(Q, 1, 2, 3)
         x_scale_out(1, 1)
         for j in (2, 3):
             x_turn(1, j)
@@ -282,51 +281,54 @@ def tile_attentionnet_pa_kernel(tc, x_bytes, x_scale, wq, wk, out):
         x_quant(1, 2, 2)
         p_quant(Q, 0, 0, 2, 2 * F)
 
-        for i in range(J + 2):
-            m, j = (K, i) if i < J else (Q, i - J)
-            project(m, 0, 1, j)
-            if i == J + 1:
-                p_quant(Q, 0, 1, 0, F)
+        for i in range(J):
+            project(K, 0, 1, i)
             if i >= 2:
                 row_out(0, i - 2)
-            project(m, 1, 1, j, i in VECTOR_COPIES)
-            if 1 <= i <= J:
+            project(K, 1, 1, i, i == VECTOR_COPY)
+            if i >= 1:
                 row_exp(0, i - 1)
-            pair_done = i < J and i % 2 == 1
-            if i < J:
-                scores(0, i)
+            pair_done = i % 2 == 1
+            scores(0, i)
             if pair_done:
                 p_quant(K, 0, 1, i - 1, 2)
-            if i < J:
-                row_bias(0, i)
+            row_bias(0, i)
+            if i >= 1:
+                row_inv(0, i - 1)
             if pair_done:
                 p_quant(K, 1, 1, i - 1, 2)
-            if 1 <= i <= J:
-                row_inv(0, i - 1)
-
+        project(Q, 0, 1, 0)
+        row_out(0, 2)
+        row_exp(0, 3)
+        project(Q, 1, 1, 0, True)
+        row_inv(0, 3)
+        project(Q, 0, 1, 1)
+        p_quant(Q, 0, 1, 0, F)
+        row_out(0, 3)
+        project(Q, 1, 1, 1)
         project(Q, 0, 1, 2)
-        p_quant(Q, 0, 1, 1, F)
-        project(Q, 0, 1, 3)
         scores(1, 0)
+        p_quant(Q, 0, 1, 1, F)
         row_bias(1, 0)
-        project(Q, 1, 1, 2, True)
+        project(Q, 1, 1, 2)
         row_exp(1, 0)
+        project(Q, 0, 1, 3)
+        scores(1, 1)
+        p_quant(Q, 0, 1, 2, F)
+        row_bias(1, 1)
+        row_inv(1, 0)
         project(Q, 1, 1, 3)
         p_quant(Q, 0, 1, 3, 1)
-        p_quant(Q, 0, 1, 2, F)
-        row_inv(1, 0)
-        scores(1, 1)
-        row_bias(1, 1)
+        row_out(1, 0)
+        row_exp(1, 1)
         p_quant(Q, 1, 1, 3, 1)
         scores(1, 2)
         scores(1, 3)
-        row_exp(1, 1)
-        row_out(1, 0)
-        for j in (2, 3):
-            row_bias(1, j)
-            row_exp(1, j)
-            if j == 2:
-                row_inv(1, 1)
+        row_bias(1, 2)
+        row_exp(1, 2)
+        row_inv(1, 1)
+        row_bias(1, 3)
+        row_exp(1, 3)
         row_out(1, 1)
         for j in (2, 3):
             row_inv(1, j)

@@ -24,7 +24,7 @@ F = 2
 K, Q = 0, 1
 BANK = 512
 FIRST_WARM_UP = 320
-VECTOR_COPY = 1
+VECTOR_COPIES = ()
 
 
 def tile_attentionnet_pa_kernel(tc, x_bytes, x_scale, wq, wk, out):
@@ -37,18 +37,21 @@ def tile_attentionnet_pa_kernel(tc, x_bytes, x_scale, wq, wk, out):
         ctx.enter_context(tc.manual_schedule())
 
         xs = keep.tile([P, G, T], F32, name="xs")
-        xraw, wraw = {}, {}
+        xraw, xpair, wraw, wload = {}, {}, {}, {}
 
         def load_x(b, j0, n):
             raw = keep.tile([P, n, D], U8, name=f"xraw{b}{j0}")
             nc.sync.dma_start(out=raw[:], in_=x_bytes[b].rearrange("(r j) k -> r j k", j=J)[:, j0:j0 + n, :])
             for i in range(n):
                 xraw[b, j0 + i] = raw[:, i, :]
+            for i in range(0, n - 1, 2):
+                xpair[b, j0 + i] = raw[:, i:i + 2, :]
 
         def load_w(m, f, s0, n):
             raw = keep.tile([P, n, D], BF16, name=f"wraw{m}{f}{s0}", align_bytes=64)
             rows = (wk, wq)[m][f * 512:(f + 1) * 512, :].rearrange("(m t) k -> m t k", t=T)
             nc.sync.dma_start(out=raw[:], in_=rows[:, s0:s0 + n, :])
+            wload[m, f, s0] = raw
             for i in range(n):
                 wraw[m, f, s0 + i] = raw[:, i, :]
 
@@ -123,6 +126,17 @@ def tile_attentionnet_pa_kernel(tc, x_bytes, x_scale, wq, wk, out):
                 for u in range(2):
                     xwords[b, j, g, u] = wide[:, u, g * P:(g + 1) * P].rearrange("r p e -> r (p e)").bitcast(F32)
 
+        def widen_pair_on_vector(b, j0):
+            wide = stage.tile([P, 2, 2 * G * P, 2], BF16, name="wide2", bufs=2, align_bytes=64)
+            nc.vector.tensor_scalar(out=wide[:].rearrange("r u c e -> r c u e"),
+                                    in0=xpair[b, j0].rearrange("r j k -> r (j k)").bitcast(FP8)
+                                    .rearrange("r (c u e) -> r c u e", u=2, e=2),
+                                    scalar1=one[:], scalar2=None, op0=ALU.mult)
+            for a in range(2 * G):
+                for u in range(2):
+                    xwords[b, j0 + a // G, a % G, u] = (wide[:, u, a * P:(a + 1) * P]
+                                                        .rearrange("r p e -> r (p e)").bitcast(F32))
+
         def widen_on_scalar(b, j):
             wide = stage.tile([P, D], BF16, name="wide", align_bytes=64)
             nc.scalar.copy(out=wide[:], in_=xraw[b, j].bitcast(FP8))
@@ -148,10 +162,13 @@ def tile_attentionnet_pa_kernel(tc, x_bytes, x_scale, wq, wk, out):
 
         dealt = {}
 
-        def w_deal(m, f, s):
-            dealt[m, f, s] = stage.tile([P, G, 2, P], F32, name="dealt", align_bytes=64)
-            nc.vector.tensor_copy(out=dealt[m, f, s][:],
-                                  in_=wraw[m, f, s].bitcast(F32).rearrange("r (g p u) -> r g u p", g=G, u=2))
+        def w_deal(m, f, s0):
+            pair = stage.tile([P, 2, G, 2, P], F32, name="dealt", bufs=2, align_bytes=64)
+            nc.vector.tensor_copy(out=pair[:].rearrange("r s g u p -> r (s g) u p"),
+                                  in_=wload[m, f, s0][:].rearrange("r s k -> r (s k)").bitcast(F32)
+                                  .rearrange("r (a p u) -> r a u p", p=P, u=2))
+            for i in range(2):
+                dealt[m, f, s0 + i] = pair[:, i]
 
         def w_turn(m, f, *slots):
             for s in slots:
@@ -224,109 +241,94 @@ def tile_attentionnet_pa_kernel(tc, x_bytes, x_scale, wq, wk, out):
             widen_on_vector(0, j)
         for j in (2, 3):
             widen_on_scalar(0, j)
-        for j in (0, 1):
-            x_turn(0, j)
-            x_scale_out(0, j)
+        x_turn(0, 0)
+        x_scale_out(0, 0)
         warm_up()
+        x_turn(0, 1)
+        x_scale_out(0, 1)
+
         w_turn(K, 0, 0)
         x_turn(0, 2)
+        x_quant(0, 0, 1)
         x_scale_out(0, 2)
-        x_quant(0, 0, 2)
+        warm_up()
         w_turn(K, 0, 1)
         x_turn(0, 3)
         x_scale_out(0, 3)
-        warm_up()
+
         w_turn(K, 0, 2, 3)
         for s0 in (0, 2):
             w_quant(K, 0, s0, 2)
+        x_quant(0, 1, 1)
         x_quant(0, 2, 2)
-        for s0 in (0, 2):
-            warm_up()
-            w_turn(K, 1, s0, s0 + 1)
+        warm_up()
+        w_turn(K, 1, 0, 1)
+        warm_up()
+        w_turn(K, 1, 2, 3)
         for j in range(J):
             project(K, 0, 0, j)
-        for s in (0, 1):
-            w_deal(Q, 0, s)
+        w_deal(Q, 0, 0)
         w_quant(K, 1, 0, T)
-        for s in (2, 3):
-            w_deal(Q, 0, s)
+        w_deal(Q, 0, 2)
         w_turn(Q, 0, 0, 1, 2, 3)
-        for j in (0, 1):
-            widen_on_vector(1, j)
-        p_quant(K, 0, 0, 0, J)
+        widen_pair_on_vector(1, 0)
+        widen_pair_on_vector(1, 2)
+        for s0 in (0, 2):
+            w_deal(Q, 1, s0)
         for j in range(J):
             project(K, 1, 0, j)
-        widen_on_vector(1, 2)
+        x_turn(1, 0)
         w_quant(Q, 0, 0, T)
-        for j in (0, 1):
-            x_turn(1, j)
-        widen_on_vector(1, 3)
         x_scale_out(1, 0)
-        w_turn(Q, 1, 0, 1)
-        warm_up()
-        w_turn(Q, 1, 2, 3)
-        x_scale_out(1, 1)
-        for j in (2, 3):
+        w_turn(Q, 1, 0, 1, 2, 3)
+        for j in (1, 2, 3):
             x_turn(1, j)
-        w_quant(Q, 1, 0, T)
+        x_scale_out(1, 1)
+        for s0 in (0, 2):
+            w_quant(Q, 1, s0, 2)
         for j in (2, 3):
             x_scale_out(1, j)
-        x_quant(1, 0, 2)
-        p_quant(K, 1, 0, 0, J)
+        x_quant(1, 0, 1)
         for f in range(F):
             for j in range(J):
                 project(Q, f, 0, j)
-                if (f, j) == (1, 1):
-                    p_quant(Q, 0, 0, 0, 2 * F)
+        x_quant(1, 1, 1)
+        p_quant(K, 0, 0, 0, J)
+        p_quant(K, 1, 0, 0, J)
+        p_quant(Q, 0, 0, 0, 2 * F)
         x_quant(1, 2, 2)
-        p_quant(Q, 0, 0, 2, 2 * F)
 
-        for i in range(J):
-            project(K, 0, 1, i)
+        tiles = [(b, j) for b in range(B) for j in range(J)]
+        for i in range(2 * J):
+            m, j = (K, i) if i < J else (Q, i - J)
+            last = i == 2 * J - 1
+            if 3 <= i < 2 * J - 1:
+                row_out(*tiles[i - 3])
+            project(m, 0, 1, j, i in VECTOR_COPIES)
+            if last:
+                p_quant(Q, 0, 1, j, 1)
+                row_out(*tiles[i - 3])
+            project(m, 1, 1, j)
             if i >= 2:
-                row_out(0, i - 2)
-            project(K, 1, 1, i, i == VECTOR_COPY)
+                row_exp(*tiles[i - 2])
+            if i == 1:
+                p_quant(Q, 0, 0, 2, 2 * F)
+            if last:
+                p_quant(Q, 1, 1, j, 1)
+            elif m == Q:
+                p_quant(Q, 0, 1, j, F)
+            elif i % 2 == 1:
+                pass
             if i >= 1:
-                row_exp(0, i - 1)
-            pair_done = i % 2 == 1
-            scores(0, i)
-            if pair_done:
-                p_quant(K, 0, 1, i - 1, 2)
-            row_bias(0, i)
-            if i >= 1:
-                row_inv(0, i - 1)
-            if pair_done:
-                p_quant(K, 1, 1, i - 1, 2)
-        project(Q, 0, 1, 0)
-        row_out(0, 2)
-        row_exp(0, 3)
-        project(Q, 1, 1, 0, True)
-        row_inv(0, 3)
-        project(Q, 0, 1, 1)
-        p_quant(Q, 0, 1, 0, F)
-        row_out(0, 3)
-        project(Q, 1, 1, 1)
-        project(Q, 0, 1, 2)
-        scores(1, 0)
-        p_quant(Q, 0, 1, 1, F)
-        row_bias(1, 0)
-        project(Q, 1, 1, 2)
-        row_exp(1, 0)
-        project(Q, 0, 1, 3)
-        scores(1, 1)
-        p_quant(Q, 0, 1, 2, F)
-        row_bias(1, 1)
-        row_inv(1, 0)
-        project(Q, 1, 1, 3)
-        p_quant(Q, 0, 1, 3, 1)
-        row_out(1, 0)
-        row_exp(1, 1)
-        p_quant(Q, 1, 1, 3, 1)
-        scores(1, 2)
+                scores(*tiles[i - 1])
+                row_bias(*tiles[i - 1])
+            if i < J and i % 2 == 1:
+                for f in range(F):
+                    p_quant(K, f, 1, i - 1, 2)
+            if i >= 2:
+                row_inv(*tiles[i - 2])
         scores(1, 3)
-        row_bias(1, 2)
         row_exp(1, 2)
-        row_inv(1, 1)
         row_bias(1, 3)
         row_exp(1, 3)
         row_out(1, 1)

@@ -56,7 +56,7 @@ def tile_attentionnet_pa_kernel(tc, x_bytes, x_scale, wq, wk, out):
                 wraw[m, f, s0 + i] = raw[:, i, :]
 
         load_x(0, 0, 1)
-        nc.sync.dma_start(out=xs[:], in_=x_scale.rearrange("o i (g p t) -> p (o i g) t", g=G, t=T))
+        nc.scalar.dma_start(out=xs[:], in_=x_scale.rearrange("o i (g p t) -> p (o i g) t", g=G, t=T))
         load_x(0, 1, 1)
         load_x(0, 2, 2)
         load_w(K, 0, 0, 1)
@@ -101,7 +101,10 @@ def tile_attentionnet_pa_kernel(tc, x_bytes, x_scale, wq, wk, out):
                     tiles[2][:, first:first + n].rearrange("p a r -> p (a r)"))
 
         def new_bank():
-            return psum.tile([P, T, P], F32, name="bank")
+            return psum.tile([P, T, P], F32, name="bank", bufs=6)
+
+        def long_bank():
+            return psum.tile([P, T, P], F32, name="long_bank", bufs=2)
 
         def every_second(pairs, g, u):
             return pairs[:, 256 * g + u:256 * (g + 1):2]
@@ -144,8 +147,8 @@ def tile_attentionnet_pa_kernel(tc, x_bytes, x_scale, wq, wk, out):
                 for u in range(2):
                     xwords[b, j, g, u] = every_second(wide[:].bitcast(F32), g, u)
 
-        def x_turn(b, j):
-            xbank[b, j] = new_bank()
+        def x_turn(b, j, long=False):
+            xbank[b, j] = long_bank() if long else new_bank()
             for g in range(G):
                 for u in range(2):
                     nc.tensor.transpose(xbank[b, j][:, 2 * g + u, :], xwords[b, j, g, u], ident[:])
@@ -205,8 +208,8 @@ def tile_attentionnet_pa_kernel(tc, x_bytes, x_scale, wq, wk, out):
 
         sbank, nbias, e, tot, inv = {}, {}, {}, {}, {}
 
-        def scores(b, j):
-            sbank[b, j] = new_bank()
+        def scores(b, j, long=True):
+            sbank[b, j] = long_bank() if long else new_bank()
             for f in range(F):
                 qc, qsc = operand(pm[Q, b], p_row(Q, f, j))
                 kc, ksc = operand(pm[K, b], p_row(K, f, 0), J)
@@ -248,12 +251,12 @@ def tile_attentionnet_pa_kernel(tc, x_bytes, x_scale, wq, wk, out):
         x_scale_out(0, 1)
 
         w_turn(K, 0, 0)
-        x_turn(0, 2)
+        x_turn(0, 2, True)
         x_quant(0, 0, 1)
         x_scale_out(0, 2)
         warm_up()
         w_turn(K, 0, 1)
-        x_turn(0, 3)
+        x_turn(0, 3, True)
         x_scale_out(0, 3)
 
         w_turn(K, 0, 2, 3)
@@ -261,7 +264,6 @@ def tile_attentionnet_pa_kernel(tc, x_bytes, x_scale, wq, wk, out):
             w_quant(K, 0, s0, 2)
         x_quant(0, 1, 1)
         x_quant(0, 2, 2)
-        warm_up()
         w_turn(K, 1, 0, 1)
         warm_up()
         w_turn(K, 1, 2, 3)
@@ -282,17 +284,16 @@ def tile_attentionnet_pa_kernel(tc, x_bytes, x_scale, wq, wk, out):
         x_scale_out(1, 0)
         w_turn(Q, 1, 0, 1, 2, 3)
         for j in (1, 2, 3):
-            x_turn(1, j)
+            x_turn(1, j, j >= 2)
         x_scale_out(1, 1)
         for s0 in (0, 2):
             w_quant(Q, 1, s0, 2)
+        x_quant(1, 0, 2)
         for j in (2, 3):
             x_scale_out(1, j)
-        x_quant(1, 0, 1)
         for f in range(F):
             for j in range(J):
                 project(Q, f, 0, j)
-        x_quant(1, 1, 1)
         p_quant(K, 0, 0, 0, J)
         p_quant(K, 1, 0, 0, J)
         p_quant(Q, 0, 0, 0, 2 * F)
@@ -327,7 +328,7 @@ def tile_attentionnet_pa_kernel(tc, x_bytes, x_scale, wq, wk, out):
                     p_quant(K, f, 1, i - 1, 2)
             if i >= 2:
                 row_inv(*tiles[i - 2])
-        scores(1, 3)
+        scores(1, 3, False)
         row_exp(1, 2)
         row_bias(1, 3)
         row_exp(1, 3)

@@ -65,7 +65,8 @@ def tile_attentionnet_pa_kernel(tc, x_bytes, x_scale, wq, wk, out):
         for m, f in ((K, 1), (Q, 0)):
             for s0 in (0, 2):
                 load_w(m, f, s0, 2)
-        load_x(1, 0, J)
+        for j0 in (0, 2):
+            load_x(1, j0, 2)
         for s0 in (0, 2):
             load_w(Q, 1, s0, 2)
 
@@ -269,23 +270,23 @@ def tile_attentionnet_pa_kernel(tc, x_bytes, x_scale, wq, wk, out):
         w_turn(K, 1, 2, 3)
         for j in range(J):
             project(K, 0, 0, j)
-        w_deal(Q, 0, 0)
-        w_quant(K, 1, 0, T)
-        w_deal(Q, 0, 2)
+        for s0 in (0, 2):
+            w_deal(Q, 0, s0)
+            w_quant(K, 1, s0, 2)
         w_turn(Q, 0, 0, 1, 2, 3)
         widen_pair_on_vector(1, 0)
         widen_pair_on_vector(1, 2)
-        for s0 in (0, 2):
-            w_deal(Q, 1, s0)
+        w_deal(Q, 1, 0)
         for j in range(J):
             project(K, 1, 0, j)
-        x_turn(1, 0)
         w_quant(Q, 0, 0, T)
-        x_scale_out(1, 0)
-        w_turn(Q, 1, 0, 1, 2, 3)
-        for j in (1, 2, 3):
+        w_deal(Q, 1, 2)
+        w_turn(Q, 1, 0, 1)
+        for j in range(J):
             x_turn(1, j, j >= 2)
-        x_scale_out(1, 1)
+        w_turn(Q, 1, 2, 3)
+        for j in (0, 1):
+            x_scale_out(1, j)
         for s0 in (0, 2):
             w_quant(Q, 1, s0, 2)
         x_quant(1, 0, 2)

@@ -24,7 +24,6 @@ F = 2
 K, Q = 0, 1
 BANK = 512
 FIRST_WARM_UP = 320
-VECTOR_COPIES = ()
 
 
 def tile_attentionnet_pa_kernel(tc, x_bytes, x_scale, wq, wk, out):
@@ -168,9 +167,9 @@ def tile_attentionnet_pa_kernel(tc, x_bytes, x_scale, wq, wk, out):
 
         def w_deal(m, f, s0):
             pair = stage.tile([P, 2, G, 2, P], F32, name="dealt", bufs=2, align_bytes=64)
-            nc.vector.tensor_copy(out=pair[:].rearrange("r s g u p -> r (s g) u p"),
+            nc.vector.tensor_copy(out=pair[:].rearrange("r s g u (c i) -> r (s g) c u i", i=2),
                                   in_=wload[m, f, s0][:].rearrange("r s k -> r (s k)").bitcast(F32)
-                                  .rearrange("r (a p u) -> r a u p", p=P, u=2))
+                                  .rearrange("r (a c i u) -> r a c u i", a=2 * G, i=2, u=2))
             for i in range(2):
                 dealt[m, f, s0 + i] = pair[:, i]
 
@@ -190,7 +189,7 @@ def tile_attentionnet_pa_kernel(tc, x_bytes, x_scale, wq, wk, out):
         def w_quant(m, f, s0, n):
             quantize(wm[m, f], G * s0, G * n)
 
-        def project(m, f, b, j, on_vector=False):
+        def project(m, f, b, j):
             bank = new_bank()
             for s in range(T):
                 for g in range(G):
@@ -198,11 +197,7 @@ def tile_attentionnet_pa_kernel(tc, x_bytes, x_scale, wq, wk, out):
                     xc, xsc = operand(xm[b], G * j + g)
                     nc.tensor.matmul_mx(out=bank[:, s, :], lhsT=wc, lhsT_scale=wsc, rhs=xc, rhs_scale=xsc,
                                         start=(g == 0), stop=(g == G - 1))
-            dst = pm[m, b][0][:, p_row(m, f, j)]
-            if on_vector:
-                nc.vector.tensor_copy(out=dst, in_=bank[:].rearrange("p t n -> p n t"))
-            else:
-                nc.scalar.copy(out=dst, in_=bank[:].rearrange("p t n -> p n t"))
+            nc.scalar.copy(out=pm[m, b][0][:, p_row(m, f, j)], in_=bank[:].rearrange("p t n -> p n t"))
 
         def p_quant(m, f, b, j, n):
             quantize(pm[m, b], p_row(m, f, j), n)
@@ -268,6 +263,7 @@ def tile_attentionnet_pa_kernel(tc, x_bytes, x_scale, wq, wk, out):
         w_turn(K, 1, 0, 1)
         warm_up()
         w_turn(K, 1, 2, 3)
+
         for j in range(J):
             project(K, 0, 0, j)
         for s0 in (0, 2):
@@ -304,9 +300,9 @@ def tile_attentionnet_pa_kernel(tc, x_bytes, x_scale, wq, wk, out):
         for i in range(2 * J):
             m, j = (K, i) if i < J else (Q, i - J)
             last = i == 2 * J - 1
-            if 3 <= i < 2 * J - 1:
+            if i >= 3 and not last:
                 row_out(*tiles[i - 3])
-            project(m, 0, 1, j, i in VECTOR_COPIES)
+            project(m, 0, 1, j)
             if last:
                 p_quant(Q, 0, 1, j, 1)
                 row_out(*tiles[i - 3])
@@ -319,12 +315,10 @@ def tile_attentionnet_pa_kernel(tc, x_bytes, x_scale, wq, wk, out):
                 p_quant(Q, 1, 1, j, 1)
             elif m == Q:
                 p_quant(Q, 0, 1, j, F)
-            elif i % 2 == 1:
-                pass
             if i >= 1:
                 scores(*tiles[i - 1])
                 row_bias(*tiles[i - 1])
-            if i < J and i % 2 == 1:
+            if m == K and i % 2 == 1:
                 for f in range(F):
                     p_quant(K, f, 1, i - 1, 2)
             if i >= 2:

@@ -76,7 +76,7 @@ def tile_attentionnet_pa_kernel(tc, x_bytes, x_scale, wq, wk, out):
         one = keep.tile([P, 1], F32, name="one")
         nc.vector.memset(one[:], 1.0)
         warm = keep.tile([P, 1], F32, name="warm")
-        nc.scalar.activation(out=warm[:], in_=one[:], func=ACT.Exp)
+        nc.scalar.activation(out=warm[:], in_=zero[:, 0:1], func=ACT.Exp)
 
         def mx_tiles(name, rows):
             return (keep.tile([P, rows, P, T], BF16, name=name + "v", align_bytes=64),
@@ -189,20 +189,25 @@ def tile_attentionnet_pa_kernel(tc, x_bytes, x_scale, wq, wk, out):
         def w_quant(m, f, s0, n):
             quantize(wm[m, f], G * s0, G * n)
 
-        def project(m, f, b, j):
-            bank = new_bank()
-            for s in range(T):
+        pbank = {}
+
+        def project(m, f, b, j, slots=range(T)):
+            if slots[0] == 0:
+                pbank[m, f, b, j] = new_bank()
+            bank = pbank[m, f, b, j]
+            for s in slots:
                 for g in range(G):
                     wc, wsc = operand(wm[m, f], G * s + g)
                     xc, xsc = operand(xm[b], G * j + g)
                     nc.tensor.matmul_mx(out=bank[:, s, :], lhsT=wc, lhsT_scale=wsc, rhs=xc, rhs_scale=xsc,
                                         start=(g == 0), stop=(g == G - 1))
-            nc.scalar.copy(out=pm[m, b][0][:, p_row(m, f, j)], in_=bank[:].rearrange("p t n -> p n t"))
+            if slots[-1] == T - 1:
+                nc.scalar.copy(out=pm[m, b][0][:, p_row(m, f, j)], in_=bank[:].rearrange("p t n -> p n t"))
 
         def p_quant(m, f, b, j, n):
             quantize(pm[m, b], p_row(m, f, j), n)
 
-        sbank, nbias, e, tot, inv = {}, {}, {}, {}, {}
+        sbank, scaled, nbias, e, tot, inv = {}, {}, {}, {}, {}, {}
 
         def scores(b, j, long=True):
             sbank[b, j] = long_bank() if long else new_bank()
@@ -214,15 +219,15 @@ def tile_attentionnet_pa_kernel(tc, x_bytes, x_scale, wq, wk, out):
 
         def row_bias(b, j):
             nbias[b, j] = soft.tile([P, 1], F32, name="nbias")
-            scaled = soft.tile([P, S], F32, name="scaled", bufs=2)
-            nc.vector.tensor_scalar(out=scaled[:], in0=sbank[b, j][:].rearrange("p j r -> p (j r)"), scalar1=-SCALE,
+            scaled[b, j] = soft.tile([P, P, J], F32, name="scaled", bufs=3)
+            nc.vector.tensor_scalar(out=scaled[b, j][:], in0=sbank[b, j][:].rearrange("p j r -> p r j"), scalar1=-SCALE,
                                     scalar2=None, op0=ALU.mult, op1=ALU.min, accum_out=nbias[b, j][:])
 
         def row_exp(b, j):
             e[b, j] = soft.tile([P, P, J], F32, name="e")
             tot[b, j] = soft.tile([P, 1], F32, name="tot")
-            nc.scalar.activation(out=e[b, j][:], in_=sbank[b, j][:].rearrange("p j r -> p r j"), func=ACT.Exp,
-                                 bias=nbias[b, j][:], scale=SCALE, accum_out=tot[b, j][:])
+            nc.scalar.activation(out=e[b, j][:], in_=scaled[b, j][:], func=ACT.Exp,
+                                 bias=nbias[b, j][:], scale=-1.0, accum_out=tot[b, j][:])
 
         def row_inv(b, j):
             inv[b, j] = soft.tile([P, 1], F32, name="inv")
@@ -270,32 +275,34 @@ def tile_attentionnet_pa_kernel(tc, x_bytes, x_scale, wq, wk, out):
             w_deal(Q, 0, s0)
             w_quant(K, 1, s0, 2)
         w_turn(Q, 0, 0, 1, 2, 3)
-        widen_pair_on_vector(1, 0)
-        widen_pair_on_vector(1, 2)
-        w_deal(Q, 1, 0)
+        for n in (0, 2):
+            widen_pair_on_vector(1, n)
+            w_deal(Q, 1, n)
         for j in range(J):
             project(K, 1, 0, j)
         w_quant(Q, 0, 0, T)
-        w_deal(Q, 1, 2)
         w_turn(Q, 1, 0, 1)
-        for j in range(J):
-            x_turn(1, j, j >= 2)
+        x_turn(1, 0)
+        for j in (2, 3):
+            x_turn(1, j, True)
         w_turn(Q, 1, 2, 3)
+        x_turn(1, 1)
         for j in (0, 1):
             x_scale_out(1, j)
-        for s0 in (0, 2):
-            w_quant(Q, 1, s0, 2)
+            w_quant(Q, 1, 2 * j, 2)
         x_quant(1, 0, 2)
-        for j in (2, 3):
-            x_scale_out(1, j)
-        for f in range(F):
-            for j in range(J):
-                project(Q, f, 0, j)
-        p_quant(K, 0, 0, 0, J)
-        p_quant(K, 1, 0, 0, J)
+        x_scale_out(1, 2)
+        for j in range(J):
+            project(Q, 0, 0, j)
+        for slots in ((0, 1), (2, 3)):
+            for j in range(3):
+                project(Q, 1, 0, j, slots)
+        for j in range(3, J):
+            project(Q, 1, 0, j)
+        p_quant(K, 0, 0, 0, F * J)
         p_quant(Q, 0, 0, 0, 2 * F)
-        x_quant(1, 2, 2)
-
+        x_quant(1, 2, 1)
+        x_scale_out(1, 3)
         tiles = [(b, j) for b in range(B) for j in range(J)]
         for i in range(2 * J):
             m, j = (K, i) if i < J else (Q, i - J)
@@ -310,7 +317,10 @@ def tile_attentionnet_pa_kernel(tc, x_bytes, x_scale, wq, wk, out):
             if i >= 2:
                 row_exp(*tiles[i - 2])
             if i == 1:
-                p_quant(Q, 0, 0, 2, 2 * F)
+                p_quant(Q, 0, 0, 2, F)
+                x_quant(1, 3, 1)
+            if i == 2:
+                p_quant(Q, 0, 0, 3, F)
             if last:
                 p_quant(Q, 1, 1, j, 1)
             elif m == Q:

@@ -23,7 +23,8 @@ J = 4
 F = 2
 K, Q = 0, 1
 BANK = 512
-FIRST_WARM_UP = 320
+FIRST_WARM_UP = 224
+SPLIT_BANKS = 3
 
 
 def tile_attentionnet_pa_kernel(tc, x_bytes, x_scale, wq, wk, out):
@@ -69,10 +70,11 @@ def tile_attentionnet_pa_kernel(tc, x_bytes, x_scale, wq, wk, out):
         for s0 in (0, 2):
             load_w(Q, 1, s0, 2)
 
-        zero = keep.tile([P, FIRST_WARM_UP], F32, name="zero")
+        zero = keep.tile([P, BANK // 2], F32, name="zero")
         nc.gpsimd.memset(zero[:], 0.0)
         ident = keep.tile([P, P], F32, name="ident")
-        make_identity(nc, ident[:])
+        nc.vector.memset(ident[:], 0.0)
+        make_identity(nc, ident[:], nomemset=True)
         one = keep.tile([P, 1], F32, name="one")
         nc.vector.memset(one[:], 1.0)
         warm = keep.tile([P, 1], F32, name="warm")
@@ -111,7 +113,7 @@ def tile_attentionnet_pa_kernel(tc, x_bytes, x_scale, wq, wk, out):
 
         def first_warm_up():
             nc.tensor.matmul(new_bank()[:].rearrange("p t n -> p (t n)")[:, 0:FIRST_WARM_UP],
-                             lhsT=zero[:, 0:P], rhs=zero[:], start=True, stop=True)
+                             lhsT=zero[:, 0:P], rhs=zero[:, 0:FIRST_WARM_UP], start=True, stop=True)
 
         def warm_up():
             zero16 = zero[:].bitcast(BF16)
@@ -275,9 +277,9 @@ def tile_attentionnet_pa_kernel(tc, x_bytes, x_scale, wq, wk, out):
             w_deal(Q, 0, s0)
             w_quant(K, 1, s0, 2)
         w_turn(Q, 0, 0, 1, 2, 3)
-        for n in (0, 2):
-            widen_pair_on_vector(1, n)
-            w_deal(Q, 1, n)
+        for first in (0, 2):
+            widen_pair_on_vector(1, first)
+            w_deal(Q, 1, first)
         for j in range(J):
             project(K, 1, 0, j)
         w_quant(Q, 0, 0, T)
@@ -295,14 +297,15 @@ def tile_attentionnet_pa_kernel(tc, x_bytes, x_scale, wq, wk, out):
         for j in range(J):
             project(Q, 0, 0, j)
         for slots in ((0, 1), (2, 3)):
-            for j in range(3):
+            for j in range(SPLIT_BANKS):
                 project(Q, 1, 0, j, slots)
-        for j in range(3, J):
+        for j in range(SPLIT_BANKS, J):
             project(Q, 1, 0, j)
         p_quant(K, 0, 0, 0, F * J)
         p_quant(Q, 0, 0, 0, 2 * F)
         x_quant(1, 2, 1)
         x_scale_out(1, 3)
+
         tiles = [(b, j) for b in range(B) for j in range(J)]
         for i in range(2 * J):
             m, j = (K, i) if i < J else (Q, i - J)
@@ -316,11 +319,10 @@ def tile_attentionnet_pa_kernel(tc, x_bytes, x_scale, wq, wk, out):
             project(m, 1, 1, j)
             if i >= 2:
                 row_exp(*tiles[i - 2])
+            if i in (1, 2):
+                p_quant(Q, 0, 0, i + 1, F)
             if i == 1:
-                p_quant(Q, 0, 0, 2, F)
                 x_quant(1, 3, 1)
-            if i == 2:
-                p_quant(Q, 0, 0, 3, F)
             if last:
                 p_quant(Q, 1, 1, j, 1)
             elif m == Q:

@@ -102,22 +102,19 @@ def tile_attentionnet_pa_kernel(tc, x_bytes, x_scale, wq, wk, out):
             return (tiles[1][:, first:first + n].rearrange("p a r -> p (a r)").bitcast(FP8X4),
                     tiles[2][:, first:first + n].rearrange("p a r -> p (a r)"))
 
-        def new_bank():
-            return psum.tile([P, T, P], F32, name="bank", bufs=6)
-
-        def long_bank():
-            return psum.tile([P, T, P], F32, name="long_bank", bufs=2)
+        def new_bank(n):
+            return psum.tile([P, T, P], F32, name=f"bank{n}", bufs=1)
 
         def every_second(pairs, g, u):
             return pairs[:, 256 * g + u:256 * (g + 1):2]
 
-        def first_warm_up():
-            nc.tensor.matmul(new_bank()[:].rearrange("p t n -> p (t n)")[:, 0:FIRST_WARM_UP],
+        def first_warm_up(n):
+            nc.tensor.matmul(new_bank(n)[:].rearrange("p t n -> p (t n)")[:, 0:FIRST_WARM_UP],
                              lhsT=zero[:, 0:P], rhs=zero[:, 0:FIRST_WARM_UP], start=True, stop=True)
 
-        def warm_up():
+        def warm_up(n):
             zero16 = zero[:].bitcast(BF16)
-            nc.tensor.matmul(new_bank()[:].rearrange("p t n -> p (t n)"),
+            nc.tensor.matmul(new_bank(n)[:].rearrange("p t n -> p (t n)"),
                              lhsT=zero16[:, 0:P], rhs=zero16[:, 0:BANK], start=True, stop=True)
 
         xwords, xbank = {}, {}
@@ -142,15 +139,27 @@ def tile_attentionnet_pa_kernel(tc, x_bytes, x_scale, wq, wk, out):
                     xwords[b, j0 + a // G, a % G, u] = (wide[:, u, a * P:(a + 1) * P]
                                                         .rearrange("r p e -> r (p e)").bitcast(F32))
 
-        def widen_on_scalar(b, j):
+        def widen_halves(b, j):
+            codes = xraw[b, j].bitcast(FP8)
+            first = stage.tile([P, 2, P, 2], BF16, name="first_half", bufs=1, align_bytes=64)
+            nc.vector.tensor_scalar(out=first[:].rearrange("r u c e -> r c u e"),
+                                    in0=codes[:, 0:512].rearrange("r (c u e) -> r c u e", u=2, e=2),
+                                    scalar1=one[:], scalar2=None, op0=ALU.mult)
+            second = stage.tile([P, 512], BF16, name="second_half", bufs=1, align_bytes=64)
+            nc.scalar.copy(out=second[:], in_=codes[:, 512:1024])
+            for u in range(2):
+                xwords[b, j, 0, u] = first[:, u].rearrange("r p e -> r (p e)").bitcast(F32)
+                xwords[b, j, 1, u] = every_second(second[:].bitcast(F32), 0, u)
+
+        def widen_plain_on_scalar(b, j):
             wide = stage.tile([P, D], BF16, name="wide", align_bytes=64)
             nc.scalar.copy(out=wide[:], in_=xraw[b, j].bitcast(FP8))
             for g in range(G):
                 for u in range(2):
                     xwords[b, j, g, u] = every_second(wide[:].bitcast(F32), g, u)
 
-        def x_turn(b, j, long=False):
-            xbank[b, j] = long_bank() if long else new_bank()
+        def x_turn(b, j, n):
+            xbank[b, j] = new_bank(n)
             for g in range(G):
                 for u in range(2):
                     nc.tensor.transpose(xbank[b, j][:, 2 * g + u, :], xwords[b, j, g, u], ident[:])
@@ -175,27 +184,26 @@ def tile_attentionnet_pa_kernel(tc, x_bytes, x_scale, wq, wk, out):
             for i in range(2):
                 dealt[m, f, s0 + i] = pair[:, i]
 
-        def w_turn(m, f, *slots):
-            for s in slots:
-                bank = new_bank()
-                for g in range(G):
-                    for u in range(2):
-                        if (m, f, s) in dealt:
-                            view = dealt[m, f, s][:, g, u, :]
-                        else:
-                            view = every_second(wraw[m, f, s].bitcast(F32), g, u)
-                        nc.tensor.transpose(bank[:, 2 * g + u, :], view, ident[:])
-                nc.scalar.copy(out=wm[m, f][0][:, G * s:G * (s + 1)].bitcast(F32),
-                               in_=bank[:].rearrange("p (g u) r -> p g r u", u=2))
+        def w_turn(m, f, s, n):
+            bank = new_bank(n)
+            for g in range(G):
+                for u in range(2):
+                    if (m, f, s) in dealt:
+                        view = dealt[m, f, s][:, g, u, :]
+                    else:
+                        view = every_second(wraw[m, f, s].bitcast(F32), g, u)
+                    nc.tensor.transpose(bank[:, 2 * g + u, :], view, ident[:])
+            nc.scalar.copy(out=wm[m, f][0][:, G * s:G * (s + 1)].bitcast(F32),
+                           in_=bank[:].rearrange("p (g u) r -> p g r u", u=2))
 
         def w_quant(m, f, s0, n):
             quantize(wm[m, f], G * s0, G * n)
 
         pbank = {}
 
-        def project(m, f, b, j, slots=range(T)):
+        def project(m, f, b, j, n, slots=range(T)):
             if slots[0] == 0:
-                pbank[m, f, b, j] = new_bank()
+                pbank[m, f, b, j] = new_bank(n)
             bank = pbank[m, f, b, j]
             for s in slots:
                 for g in range(G):
@@ -211,8 +219,8 @@ def tile_attentionnet_pa_kernel(tc, x_bytes, x_scale, wq, wk, out):
 
         sbank, scaled, nbias, e, tot, inv = {}, {}, {}, {}, {}, {}
 
-        def scores(b, j, long=True):
-            sbank[b, j] = long_bank() if long else new_bank()
+        def scores(b, j, n):
+            sbank[b, j] = new_bank(n)
             for f in range(F):
                 qc, qsc = operand(pm[Q, b], p_row(Q, f, j))
                 kc, ksc = operand(pm[K, b], p_row(K, f, 0), J)
@@ -241,82 +249,84 @@ def tile_attentionnet_pa_kernel(tc, x_bytes, x_scale, wq, wk, out):
                                     scalar2=None, op0=ALU.mult)
             nc.sync.dma_start(out=out[b].rearrange("(r j) s -> r j s", j=J)[:, j, :], in_=prob[:])
 
-        first_warm_up()
-        first_warm_up()
-        for j in (0, 1):
-            widen_on_vector(0, j)
+        first_warm_up(0)
+        first_warm_up(1)
+        widen_halves(0, 0)
+        widen_on_vector(0, 1)
         for j in (2, 3):
-            widen_on_scalar(0, j)
-        x_turn(0, 0)
+            widen_plain_on_scalar(0, j)
+        x_turn(0, 0, 2)
         x_scale_out(0, 0)
-        warm_up()
-        x_turn(0, 1)
+        warm_up(3)
+        x_turn(0, 1, 4)
         x_scale_out(0, 1)
-
-        w_turn(K, 0, 0)
-        x_turn(0, 2, True)
+        w_turn(K, 0, 0, 5)
+        x_turn(0, 2, 6)
         x_quant(0, 0, 1)
         x_scale_out(0, 2)
-        warm_up()
-        w_turn(K, 0, 1)
-        x_turn(0, 3, True)
+        warm_up(0)
+        w_turn(K, 0, 1, 1)
+        x_turn(0, 3, 7)
+        w_turn(K, 0, 2, 2)
+        w_turn(K, 0, 3, 3)
         x_scale_out(0, 3)
-
-        w_turn(K, 0, 2, 3)
         for s0 in (0, 2):
             w_quant(K, 0, s0, 2)
         x_quant(0, 1, 1)
         x_quant(0, 2, 2)
-        w_turn(K, 1, 0, 1)
-        warm_up()
-        w_turn(K, 1, 2, 3)
-
+        w_turn(K, 1, 0, 4)
+        w_turn(K, 1, 1, 5)
+        warm_up(0)
+        w_turn(K, 1, 2, 1)
+        w_turn(K, 1, 3, 2)
         for j in range(J):
-            project(K, 0, 0, j)
+            project(K, 0, 0, j, (3 + j) % 6)
         for s0 in (0, 2):
             w_deal(Q, 0, s0)
             w_quant(K, 1, s0, 2)
-        w_turn(Q, 0, 0, 1, 2, 3)
+        for s in range(T):
+            w_turn(Q, 0, s, 1 + s)
         for first in (0, 2):
             widen_pair_on_vector(1, first)
             w_deal(Q, 1, first)
         for j in range(J):
-            project(K, 1, 0, j)
+            project(K, 1, 0, j, (5 + j) % 6)
         w_quant(Q, 0, 0, T)
-        w_turn(Q, 1, 0, 1)
-        x_turn(1, 0)
-        for j in (2, 3):
-            x_turn(1, j, True)
-        w_turn(Q, 1, 2, 3)
-        x_turn(1, 1)
+        w_turn(Q, 1, 0, 3)
+        w_turn(Q, 1, 1, 4)
+        x_turn(1, 0, 5)
+        x_turn(1, 2, 6)
+        x_turn(1, 3, 7)
+        w_turn(Q, 1, 2, 0)
+        w_turn(Q, 1, 3, 1)
+        x_turn(1, 1, 2)
         for j in (0, 1):
             x_scale_out(1, j)
             w_quant(Q, 1, 2 * j, 2)
         x_quant(1, 0, 2)
         x_scale_out(1, 2)
         for j in range(J):
-            project(Q, 0, 0, j)
+            project(Q, 0, 0, j, (3 + j) % 6)
         for slots in ((0, 1), (2, 3)):
             for j in range(SPLIT_BANKS):
-                project(Q, 1, 0, j, slots)
+                project(Q, 1, 0, j, 1 + j, slots)
         for j in range(SPLIT_BANKS, J):
-            project(Q, 1, 0, j)
+            project(Q, 1, 0, j, 1 + j)
         p_quant(K, 0, 0, 0, F * J)
         p_quant(Q, 0, 0, 0, 2 * F)
         x_quant(1, 2, 1)
         x_scale_out(1, 3)
-
         tiles = [(b, j) for b in range(B) for j in range(J)]
         for i in range(2 * J):
             m, j = (K, i) if i < J else (Q, i - J)
             last = i == 2 * J - 1
             if i >= 3 and not last:
                 row_out(*tiles[i - 3])
-            project(m, 0, 1, j)
+            project(m, 0, 1, j, (2 * i + 5) % 6)
             if last:
                 p_quant(Q, 0, 1, j, 1)
                 row_out(*tiles[i - 3])
-            project(m, 1, 1, j)
+            project(m, 1, 1, j, (2 * i + 6) % 6)
             if i >= 2:
                 row_exp(*tiles[i - 2])
             if i in (1, 2):
@@ -328,14 +338,14 @@ def tile_attentionnet_pa_kernel(tc, x_bytes, x_scale, wq, wk, out):
             elif m == Q:
                 p_quant(Q, 0, 1, j, F)
             if i >= 1:
-                scores(*tiles[i - 1])
+                scores(*tiles[i - 1], 7 - i % 2)
                 row_bias(*tiles[i - 1])
+            if i >= 2:
+                row_inv(*tiles[i - 2])
             if m == K and i % 2 == 1:
                 for f in range(F):
                     p_quant(K, f, 1, i - 1, 2)
-            if i >= 2:
-                row_inv(*tiles[i - 2])
-        scores(1, 3, False)
+        scores(1, 3, 3)
         row_exp(1, 2)
         row_bias(1, 3)
         row_exp(1, 3)

@@ -75,8 +75,6 @@ def tile_attentionnet_pa_kernel(tc, x_bytes, x_scale, wq, wk, out):
         ident = keep.tile([P, P], F32, name="ident")
         nc.vector.memset(ident[:], 0.0)
         make_identity(nc, ident[:], nomemset=True)
-        one = keep.tile([P, 1], F32, name="one")
-        nc.vector.memset(one[:], 1.0)
         warm = keep.tile([P, 1], F32, name="warm")
         nc.scalar.activation(out=warm[:], in_=zero[:, 0:1], func=ACT.Exp)
 
@@ -121,19 +119,17 @@ def tile_attentionnet_pa_kernel(tc, x_bytes, x_scale, wq, wk, out):
 
         def widen_on_vector(b, j):
             wide = stage.tile([P, 2, G * P, 2], BF16, name="wide", align_bytes=64)
-            nc.vector.tensor_scalar(out=wide[:].rearrange("r u c e -> r c u e"),
-                                    in0=xraw[b, j].bitcast(FP8).rearrange("r (c u e) -> r c u e", u=2, e=2),
-                                    scalar1=one[:], scalar2=None, op0=ALU.mult)
+            nc.vector.tensor_copy(out=wide[:].rearrange("r u c e -> r c u e"),
+                                  in_=xraw[b, j].bitcast(FP8).rearrange("r (c u e) -> r c u e", u=2, e=2))
             for g in range(G):
                 for u in range(2):
                     xwords[b, j, g, u] = wide[:, u, g * P:(g + 1) * P].rearrange("r p e -> r (p e)").bitcast(F32)
 
         def widen_pair_on_vector(b, j0):
             wide = stage.tile([P, 2, 2 * G * P, 2], BF16, name="wide2", bufs=2, align_bytes=64)
-            nc.vector.tensor_scalar(out=wide[:].rearrange("r u c e -> r c u e"),
-                                    in0=xpair[b, j0].rearrange("r j k -> r (j k)").bitcast(FP8)
-                                    .rearrange("r (c u e) -> r c u e", u=2, e=2),
-                                    scalar1=one[:], scalar2=None, op0=ALU.mult)
+            nc.vector.tensor_copy(out=wide[:].rearrange("r u c e -> r c u e"),
+                                  in_=xpair[b, j0].rearrange("r j k -> r (j k)").bitcast(FP8)
+                                    .rearrange("r (c u e) -> r c u e", u=2, e=2))
             for a in range(2 * G):
                 for u in range(2):
                     xwords[b, j0 + a // G, a % G, u] = (wide[:, u, a * P:(a + 1) * P]
@@ -142,9 +138,8 @@ def tile_attentionnet_pa_kernel(tc, x_bytes, x_scale, wq, wk, out):
         def widen_halves(b, j):
             codes = xraw[b, j].bitcast(FP8)
             first = stage.tile([P, 2, P, 2], BF16, name="first_half", bufs=1, align_bytes=64)
-            nc.vector.tensor_scalar(out=first[:].rearrange("r u c e -> r c u e"),
-                                    in0=codes[:, 0:512].rearrange("r (c u e) -> r c u e", u=2, e=2),
-                                    scalar1=one[:], scalar2=None, op0=ALU.mult)
+            nc.vector.tensor_copy(out=first[:].rearrange("r u c e -> r c u e"),
+                                  in_=codes[:, 0:512].rearrange("r (c u e) -> r c u e", u=2, e=2))
             second = stage.tile([P, 512], BF16, name="second_half", bufs=1, align_bytes=64)
             nc.scalar.copy(out=second[:], in_=codes[:, 512:1024])
             for u in range(2):
@@ -162,13 +157,13 @@ def tile_attentionnet_pa_kernel(tc, x_bytes, x_scale, wq, wk, out):
             xbank[b, j] = new_bank(n)
             for g in range(G):
                 for u in range(2):
-                    nc.tensor.transpose(xbank[b, j][:, 2 * g + u, :], xwords[b, j, g, u], ident[:])
+                    nc.tensor.transpose(xbank[b, j][:, G * u + g, :], xwords[b, j, g, u], ident[:])
 
         def x_scale_out(b, j):
             nc.vector.tensor_tensor(
-                out=xm[b][0][:, G * j:G * (j + 1)].rearrange("p g r (u e) -> p r g u e", u=2),
-                in0=xbank[b, j][:].bitcast(BF16).rearrange("p (g u) (r e) -> p r g u e", u=2, e=2),
-                in1=xs[:].rearrange("p g (u e) -> p g u e", u=2).unsqueeze(1).to_broadcast([P, P, G, 2, 2]),
+                out=xm[b][0][:, G * j:G * (j + 1)].rearrange("p g r (u e) -> p g r u e", u=2),
+                in0=xbank[b, j][:].bitcast(BF16).rearrange("p (u g) (r e) -> p g r u e", u=2, e=2),
+                in1=xs[:].rearrange("p g (u e) -> p g u e", u=2).unsqueeze(2).to_broadcast([P, G, P, 2, 2]),
                 op=ALU.mult)
 
         def x_quant(b, j0, n):

@@ -24,6 +24,7 @@ F = 2
 K, Q = 0, 1
 BANK = 512
 FIRST_WARM_UP = 224
+LAST_ON_VECTOR = 352
 SPLIT_BANKS = 3
 
 
@@ -238,10 +239,14 @@ def tile_attentionnet_pa_kernel(tc, x_bytes, x_scale, wq, wk, out):
             inv[b, j] = soft.tile([P, 1], F32, name="inv")
             nc.vector.reciprocal(out=inv[b, j][:], in_=tot[b, j][:])
 
-        def row_out(b, j):
+        def row_out(b, j, on_vector=S):
             prob = soft.tile([P, S], F32, name="prob", bufs=5)
-            nc.vector.tensor_scalar(out=prob[:], in0=e[b, j][:].rearrange("p r j -> p (r j)"), scalar1=inv[b, j][:],
-                                    scalar2=None, op0=ALU.mult)
+            rows = e[b, j][:].rearrange("p r j -> p (r j)")
+            if on_vector > 0:
+                nc.vector.tensor_scalar(out=prob[:, :on_vector], in0=rows[:, :on_vector], scalar1=inv[b, j][:],
+                                        scalar2=None, op0=ALU.mult)
+            if on_vector < S:
+                nc.scalar.activation(out=prob[:, on_vector:], in_=rows[:, on_vector:], func=ACT.Copy, scale=inv[b, j][:])
             nc.sync.dma_start(out=out[b].rearrange("(r j) s -> r j s", j=J)[:, j, :], in_=prob[:])
 
         first_warm_up(0)
@@ -315,12 +320,11 @@ def tile_attentionnet_pa_kernel(tc, x_bytes, x_scale, wq, wk, out):
         for i in range(2 * J):
             m, j = (K, i) if i < J else (Q, i - J)
             last = i == 2 * J - 1
-            if i >= 3 and not last:
+            if 4 <= i < 2 * J - 1:
                 row_out(*tiles[i - 3])
             project(m, 0, 1, j, (2 * i + 5) % 6)
             if last:
                 p_quant(Q, 0, 1, j, 1)
-                row_out(*tiles[i - 3])
             project(m, 1, 1, j, (2 * i + 6) % 6)
             if i >= 2:
                 row_exp(*tiles[i - 2])
@@ -335,16 +339,19 @@ def tile_attentionnet_pa_kernel(tc, x_bytes, x_scale, wq, wk, out):
             if i >= 1:
                 scores(*tiles[i - 1], 7 - i % 2)
                 row_bias(*tiles[i - 1])
+            if 3 <= i < 4:
+                row_out(*tiles[i - 3])
             if i >= 2:
                 row_inv(*tiles[i - 2])
             if m == K and i % 2 == 1:
                 for f in range(F):
                     p_quant(K, f, 1, i - 1, 2)
         scores(1, 3, 3)
+        row_out(1, 0, 0)
         row_exp(1, 2)
         row_bias(1, 3)
         row_exp(1, 3)
         row_out(1, 1)
         for j in (2, 3):
             row_inv(1, j)
-            row_out(1, j)
+            row_out(1, j, LAST_ON_VECTOR if j == J - 1 else S)

@@ -42,7 +42,7 @@ def tile_attentionnet_pa_kernel(tc, x_bytes, x_scale, wq, wk, out):
 
         def load_x(b, j0, n):
             raw = keep.tile([P, n, D], U8, name=f"xraw{b}{j0}")
-            nc.sync.dma_start(out=raw[:], in_=x_bytes[b].rearrange("(r j) k -> r j k", j=J)[:, j0:j0 + n, :])
+            nc.sync.dma_start(out=raw[:], in_=x_bytes[b].rearrange("(j r) k -> r j k", j=J)[:, j0:j0 + n, :])
             for i in range(n):
                 xraw[b, j0 + i] = raw[:, i, :]
             for i in range(0, n - 1, 2):
@@ -225,12 +225,12 @@ def tile_attentionnet_pa_kernel(tc, x_bytes, x_scale, wq, wk, out):
 
         def row_bias(b, j):
             nbias[b, j] = soft.tile([P, 1], F32, name="nbias")
-            scaled[b, j] = soft.tile([P, P, J], F32, name="scaled", bufs=3)
-            nc.vector.tensor_scalar(out=scaled[b, j][:], in0=sbank[b, j][:].rearrange("p j r -> p r j"), scalar1=-SCALE,
+            scaled[b, j] = soft.tile([P, S], F32, name="scaled", bufs=3)
+            nc.vector.tensor_scalar(out=scaled[b, j][:], in0=sbank[b, j][:].rearrange("p j r -> p (j r)"), scalar1=-SCALE,
                                     scalar2=None, op0=ALU.mult, op1=ALU.min, accum_out=nbias[b, j][:])
 
         def row_exp(b, j):
-            e[b, j] = soft.tile([P, P, J], F32, name="e")
+            e[b, j] = soft.tile([P, S], F32, name="e")
             tot[b, j] = soft.tile([P, 1], F32, name="tot")
             nc.scalar.activation(out=e[b, j][:], in_=scaled[b, j][:], func=ACT.Exp,
                                  bias=nbias[b, j][:], scale=-1.0, accum_out=tot[b, j][:])
@@ -241,13 +241,13 @@ def tile_attentionnet_pa_kernel(tc, x_bytes, x_scale, wq, wk, out):
 
         def row_out(b, j, on_vector=S):
             prob = soft.tile([P, S], F32, name="prob", bufs=5)
-            rows = e[b, j][:].rearrange("p r j -> p (r j)")
+            rows = e[b, j]
             if on_vector > 0:
                 nc.vector.tensor_scalar(out=prob[:, :on_vector], in0=rows[:, :on_vector], scalar1=inv[b, j][:],
                                         scalar2=None, op0=ALU.mult)
             if on_vector < S:
                 nc.scalar.activation(out=prob[:, on_vector:], in_=rows[:, on_vector:], func=ACT.Copy, scale=inv[b, j][:])
-            nc.sync.dma_start(out=out[b].rearrange("(r j) s -> r j s", j=J)[:, j, :], in_=prob[:])
+            nc.sync.dma_start(out=out[b, P * j:P * (j + 1), :], in_=prob[:])
 
         first_warm_up(0)
         first_warm_up(1)

@@ -25,7 +25,6 @@ K, Q = 0, 1
 BANK = 512
 FIRST_WARM_UP = 224
 LAST_ON_VECTOR = 352
-SPLIT_BANKS = 3
 
 
 def tile_attentionnet_pa_kernel(tc, x_bytes, x_scale, wq, wk, out):
@@ -42,7 +41,7 @@ def tile_attentionnet_pa_kernel(tc, x_bytes, x_scale, wq, wk, out):
 
         def load_x(b, j0, n):
             raw = keep.tile([P, n, D], U8, name=f"xraw{b}{j0}")
-            nc.sync.dma_start(out=raw[:], in_=x_bytes[b].rearrange("(j r) k -> r j k", j=J)[:, j0:j0 + n, :])
+            nc.sync.dma_start(out=raw[:], in_=x_bytes[b].rearrange("(h r i) k -> h r i k", h=2, i=2)[j0 // 2, :, j0 % 2:j0 % 2 + n, :])
             for i in range(n):
                 xraw[b, j0 + i] = raw[:, i, :]
             for i in range(0, n - 1, 2):
@@ -195,20 +194,15 @@ def tile_attentionnet_pa_kernel(tc, x_bytes, x_scale, wq, wk, out):
         def w_quant(m, f, s0, n):
             quantize(wm[m, f], G * s0, G * n)
 
-        pbank = {}
-
-        def project(m, f, b, j, n, slots=range(T)):
-            if slots[0] == 0:
-                pbank[m, f, b, j] = new_bank(n)
-            bank = pbank[m, f, b, j]
-            for s in slots:
+        def project(m, f, b, j, n):
+            bank = new_bank(n)
+            for s in range(T):
                 for g in range(G):
                     wc, wsc = operand(wm[m, f], G * s + g)
                     xc, xsc = operand(xm[b], G * j + g)
                     nc.tensor.matmul_mx(out=bank[:, s, :], lhsT=wc, lhsT_scale=wsc, rhs=xc, rhs_scale=xsc,
                                         start=(g == 0), stop=(g == G - 1))
-            if slots[-1] == T - 1:
-                nc.scalar.copy(out=pm[m, b][0][:, p_row(m, f, j)], in_=bank[:].rearrange("p t n -> p n t"))
+            nc.scalar.copy(out=pm[m, b][0][:, p_row(m, f, j)], in_=bank[:].rearrange("p t n -> p n t"))
 
         def p_quant(m, f, b, j, n):
             quantize(pm[m, b], p_row(m, f, j), n)
@@ -225,12 +219,12 @@ def tile_attentionnet_pa_kernel(tc, x_bytes, x_scale, wq, wk, out):
 
         def row_bias(b, j):
             nbias[b, j] = soft.tile([P, 1], F32, name="nbias")
-            scaled[b, j] = soft.tile([P, S], F32, name="scaled", bufs=3)
-            nc.vector.tensor_scalar(out=scaled[b, j][:], in0=sbank[b, j][:].rearrange("p j r -> p (j r)"), scalar1=-SCALE,
+            scaled[b, j] = soft.tile([P, 2, P, 2], F32, name="scaled", bufs=3)
+            nc.vector.tensor_scalar(out=scaled[b, j][:], in0=sbank[b, j][:].rearrange("p (h i) r -> p h r i", i=2), scalar1=-SCALE,
                                     scalar2=None, op0=ALU.mult, op1=ALU.min, accum_out=nbias[b, j][:])
 
         def row_exp(b, j):
-            e[b, j] = soft.tile([P, S], F32, name="e")
+            e[b, j] = soft.tile([P, 2, P, 2], F32, name="e")
             tot[b, j] = soft.tile([P, 1], F32, name="tot")
             nc.scalar.activation(out=e[b, j][:], in_=scaled[b, j][:], func=ACT.Exp,
                                  bias=nbias[b, j][:], scale=-1.0, accum_out=tot[b, j][:])
@@ -241,13 +235,13 @@ def tile_attentionnet_pa_kernel(tc, x_bytes, x_scale, wq, wk, out):
 
         def row_out(b, j, on_vector=S):
             prob = soft.tile([P, S], F32, name="prob", bufs=5)
-            rows = e[b, j]
+            rows = e[b, j][:].rearrange("p h r i -> p (h r i)")
             if on_vector > 0:
                 nc.vector.tensor_scalar(out=prob[:, :on_vector], in0=rows[:, :on_vector], scalar1=inv[b, j][:],
                                         scalar2=None, op0=ALU.mult)
             if on_vector < S:
                 nc.scalar.activation(out=prob[:, on_vector:], in_=rows[:, on_vector:], func=ACT.Copy, scale=inv[b, j][:])
-            nc.sync.dma_start(out=out[b, P * j:P * (j + 1), :], in_=prob[:])
+            nc.sync.dma_start(out=out[b].rearrange("(h r i) s -> h i r s", h=2, i=2)[j // 2, j % 2], in_=prob[:])
 
         first_warm_up(0)
         first_warm_up(1)
@@ -300,19 +294,19 @@ def tile_attentionnet_pa_kernel(tc, x_bytes, x_scale, wq, wk, out):
         w_turn(Q, 1, 2, 0)
         w_turn(Q, 1, 3, 1)
         x_turn(1, 1, 2)
-        for j in (0, 1):
-            x_scale_out(1, j)
-            w_quant(Q, 1, 2 * j, 2)
+        x_scale_out(1, 0)
+        for s0 in (0, 2):
+            w_quant(Q, 1, s0, 2)
+        x_scale_out(1, 1)
+        p_quant(K, 0, 0, 0, J)
         x_quant(1, 0, 2)
         x_scale_out(1, 2)
         for j in range(J):
             project(Q, 0, 0, j, (3 + j) % 6)
-        for slots in ((0, 1), (2, 3)):
-            for j in range(SPLIT_BANKS):
-                project(Q, 1, 0, j, 1 + j, slots)
-        for j in range(SPLIT_BANKS, J):
-            project(Q, 1, 0, j, 1 + j)
-        p_quant(K, 0, 0, 0, F * J)
+        ring = (5, 0, 1, 3, 4, 2)
+        for j in range(J):
+            project(Q, 1, 0, j, ring[2 + j])
+        p_quant(K, 1, 0, 0, J)
         p_quant(Q, 0, 0, 0, 2 * F)
         x_quant(1, 2, 1)
         x_scale_out(1, 3)
@@ -322,10 +316,10 @@ def tile_attentionnet_pa_kernel(tc, x_bytes, x_scale, wq, wk, out):
             last = i == 2 * J - 1
             if 4 <= i < 2 * J - 1:
                 row_out(*tiles[i - 3])
-            project(m, 0, 1, j, (2 * i + 5) % 6)
+            project(m, 0, 1, j, ring[2 * i % 6])
             if last:
                 p_quant(Q, 0, 1, j, 1)
-            project(m, 1, 1, j, (2 * i + 6) % 6)
+            project(m, 1, 1, j, ring[(2 * i + 1) % 6])
             if i >= 2:
                 row_exp(*tiles[i - 2])
             if i in (1, 2):
@@ -346,7 +340,7 @@ def tile_attentionnet_pa_kernel(tc, x_bytes, x_scale, wq, wk, out):
             if m == K and i % 2 == 1:
                 for f in range(F):
                     p_quant(K, f, 1, i - 1, 2)
-        scores(1, 3, 3)
+        scores(1, 3, ring[4])
         row_out(1, 0, 0)
         row_exp(1, 2)
         row_bias(1, 3)

@@ -166,6 +166,16 @@ def tile_attentionnet_pa_kernel(tc, x_bytes, x_scale, wq, wk, out):
                 in1=xs[:].rearrange("p g (u e) -> p g u e", u=2).unsqueeze(2).to_broadcast([P, G, P, 2, 2]),
                 op=ALU.mult)
 
+        def x_first(g, n):
+            bank = new_bank(n)
+            for u in range(2):
+                nc.tensor.transpose(bank[:, u, :], xwords[0, 0, g, u], ident[:])
+            nc.vector.tensor_tensor(
+                out=xm[0][0][:, g].rearrange("p r (u e) -> p r u e", u=2),
+                in0=bank[:, 0:2].bitcast(BF16).rearrange("p u (r e) -> p r u e", e=2),
+                in1=xs[:, g].rearrange("p (u e) -> p u e", u=2).unsqueeze(1).to_broadcast([P, P, 2, 2]),
+                op=ALU.mult)
+
         def x_quant(b, j0, n):
             quantize(xm[b], G * j0, G * n)
 
@@ -179,8 +189,16 @@ def tile_attentionnet_pa_kernel(tc, x_bytes, x_scale, wq, wk, out):
             for i in range(2):
                 dealt[m, f, s0 + i] = pair[:, i]
 
+        def w_deal_on_scalar(m, f, s):
+            slot = keep.tile([P, G, 2, P], F32, name=f"slot{m}{f}{s}", align_bytes=64)
+            nc.scalar.copy(out=slot[:].rearrange("r g u p -> r g p u"),
+                           in_=wraw[m, f, s].bitcast(F32).rearrange("r (g p u) -> r g p u", g=G, u=2))
+            dealt[m, f, s] = slot[:]
+
+        wbank, pbank = {}, {}
+
         def w_turn(m, f, s, n):
-            bank = new_bank(n)
+            bank = wbank[m, f, s] = new_bank(n)
             for g in range(G):
                 for u in range(2):
                     if (m, f, s) in dealt:
@@ -188,21 +206,33 @@ def tile_attentionnet_pa_kernel(tc, x_bytes, x_scale, wq, wk, out):
                     else:
                         view = every_second(wraw[m, f, s].bitcast(F32), g, u)
                     nc.tensor.transpose(bank[:, 2 * g + u, :], view, ident[:])
+
+        def w_copy(m, f, s):
             nc.scalar.copy(out=wm[m, f][0][:, G * s:G * (s + 1)].bitcast(F32),
-                           in_=bank[:].rearrange("p (g u) r -> p g r u", u=2))
+                           in_=wbank[m, f, s][:].rearrange("p (g u) r -> p g r u", u=2))
 
         def w_quant(m, f, s0, n):
             quantize(wm[m, f], G * s0, G * n)
 
-        def project(m, f, b, j, n):
-            bank = new_bank(n)
+        def p_mul(m, f, b, j, n):
+            bank = pbank[m, f, b, j] = new_bank(n)
             for s in range(T):
                 for g in range(G):
                     wc, wsc = operand(wm[m, f], G * s + g)
                     xc, xsc = operand(xm[b], G * j + g)
                     nc.tensor.matmul_mx(out=bank[:, s, :], lhsT=wc, lhsT_scale=wsc, rhs=xc, rhs_scale=xsc,
                                         start=(g == 0), stop=(g == G - 1))
-            nc.scalar.copy(out=pm[m, b][0][:, p_row(m, f, j)], in_=bank[:].rearrange("p t n -> p n t"))
+
+        def p_copy(m, f, b, j):
+            nc.scalar.copy(out=pm[m, b][0][:, p_row(m, f, j)], in_=pbank[m, f, b, j][:].rearrange("p t n -> p n t"))
+
+        def project(m, f, b, j, n):
+            p_mul(m, f, b, j, n)
+            p_copy(m, f, b, j)
+
+        def w_pass(m, f, s, n):
+            w_turn(m, f, s, n)
+            w_copy(m, f, s)
 
         def p_quant(m, f, b, j, n):
             quantize(pm[m, b], p_row(m, f, j), n)
@@ -249,56 +279,61 @@ def tile_attentionnet_pa_kernel(tc, x_bytes, x_scale, wq, wk, out):
         widen_on_vector(0, 1)
         for j in (2, 3):
             widen_plain_on_scalar(0, j)
-        x_turn(0, 0, 2)
-        x_scale_out(0, 0)
-        warm_up(3)
+        x_first(0, 2)
+        x_first(1, 3)
+        warm_up(0)
         x_turn(0, 1, 4)
         x_scale_out(0, 1)
-        w_turn(K, 0, 0, 5)
+        w_pass(K, 0, 0, 5)
         x_turn(0, 2, 6)
         x_quant(0, 0, 1)
         x_scale_out(0, 2)
+        w_pass(K, 0, 1, 1)
         warm_up(0)
-        w_turn(K, 0, 1, 1)
+        w_pass(K, 0, 2, 2)
+        w_pass(K, 0, 3, 3)
         x_turn(0, 3, 7)
-        w_turn(K, 0, 2, 2)
-        w_turn(K, 0, 3, 3)
-        x_scale_out(0, 3)
-        for s0 in (0, 2):
-            w_quant(K, 0, s0, 2)
+        w_quant(K, 0, 0, 2)
         x_quant(0, 1, 1)
-        x_quant(0, 2, 2)
-        w_turn(K, 1, 0, 4)
-        w_turn(K, 1, 1, 5)
+        w_quant(K, 0, 2, 2)
+        x_quant(0, 2, 1)
+        w_deal(Q, 0, 0)
+        x_scale_out(0, 3)
+        w_deal(Q, 0, 2)
+        x_quant(0, 3, 1)
+        w_deal_on_scalar(K, 1, 3)
+        w_pass(K, 1, 0, 4)
         warm_up(0)
-        w_turn(K, 1, 2, 1)
-        w_turn(K, 1, 3, 2)
-        for j in range(J):
-            project(K, 0, 0, j, (3 + j) % 6)
+        w_pass(K, 1, 1, 5)
+        w_pass(K, 1, 2, 1)
+        w_pass(K, 1, 3, 2)
+        for j in range(J - 1):
+            project(K, 0, 0, j, 3 + j)
         for s0 in (0, 2):
-            w_deal(Q, 0, s0)
             w_quant(K, 1, s0, 2)
         for s in range(T):
-            w_turn(Q, 0, s, 1 + s)
+            w_pass(Q, 0, s, s)
+        project(K, 0, 0, J - 1, 4)
         for first in (0, 2):
             widen_pair_on_vector(1, first)
             w_deal(Q, 1, first)
         for j in range(J):
             project(K, 1, 0, j, (5 + j) % 6)
         w_quant(Q, 0, 0, T)
-        w_turn(Q, 1, 0, 3)
-        w_turn(Q, 1, 1, 4)
+        w_pass(Q, 1, 0, 3)
+        w_pass(Q, 1, 1, 4)
         x_turn(1, 0, 5)
         x_turn(1, 2, 6)
         x_turn(1, 3, 7)
-        w_turn(Q, 1, 2, 0)
-        w_turn(Q, 1, 3, 1)
+        w_pass(Q, 1, 2, 0)
+        w_pass(Q, 1, 3, 1)
         x_turn(1, 1, 2)
         x_scale_out(1, 0)
-        for s0 in (0, 2):
-            w_quant(Q, 1, s0, 2)
+        w_quant(Q, 1, 0, 2)
+        p_quant(K, 0, 0, 0, 2)
+        w_quant(Q, 1, 2, 2)
         x_scale_out(1, 1)
-        p_quant(K, 0, 0, 0, J)
+        p_quant(K, 0, 0, 2, 2)
         x_quant(1, 0, 2)
         x_scale_out(1, 2)
         for j in range(J):
@@ -307,25 +342,21 @@ def tile_attentionnet_pa_kernel(tc, x_bytes, x_scale, wq, wk, out):
         for j in range(J):
             project(Q, 1, 0, j, ring[2 + j])
         p_quant(K, 1, 0, 0, J)
-        p_quant(Q, 0, 0, 0, 2 * F)
+        p_quant(Q, 0, 0, 0, F)
         x_quant(1, 2, 1)
         x_scale_out(1, 3)
+        p_quant(Q, 0, 0, 1, F)
+        x_quant(1, 3, 1)
         tiles = [(b, j) for b in range(B) for j in range(J)]
         for i in range(2 * J):
             m, j = (K, i) if i < J else (Q, i - J)
             last = i == 2 * J - 1
-            if 4 <= i < 2 * J - 1:
-                row_out(*tiles[i - 3])
             project(m, 0, 1, j, ring[2 * i % 6])
             if last:
                 p_quant(Q, 0, 1, j, 1)
             project(m, 1, 1, j, ring[(2 * i + 1) % 6])
             if i >= 2:
                 row_exp(*tiles[i - 2])
-            if i in (1, 2):
-                p_quant(Q, 0, 0, i + 1, F)
-            if i == 1:
-                x_quant(1, 3, 1)
             if last:
                 p_quant(Q, 1, 1, j, 1)
             elif m == Q:
@@ -333,13 +364,15 @@ def tile_attentionnet_pa_kernel(tc, x_bytes, x_scale, wq, wk, out):
             if i >= 1:
                 scores(*tiles[i - 1], 7 - i % 2)
                 row_bias(*tiles[i - 1])
-            if 3 <= i < 4:
-                row_out(*tiles[i - 3])
-            if i >= 2:
-                row_inv(*tiles[i - 2])
+            if i in (1, 2):
+                p_quant(Q, 0, 0, i + 1, F)
             if m == K and i % 2 == 1:
                 for f in range(F):
                     p_quant(K, f, 1, i - 1, 2)
+            if i >= 2:
+                row_inv(*tiles[i - 2])
+            if 3 <= i < 7:
+                row_out(*tiles[i - 3])
         scores(1, 3, ring[4])
         row_out(1, 0, 0)
         row_exp(1, 2)

@@ -166,16 +166,6 @@ def tile_attentionnet_pa_kernel(tc, x_bytes, x_scale, wq, wk, out):
                 in1=xs[:].rearrange("p g (u e) -> p g u e", u=2).unsqueeze(2).to_broadcast([P, G, P, 2, 2]),
                 op=ALU.mult)
 
-        def x_first(g, n):
-            bank = new_bank(n)
-            for u in range(2):
-                nc.tensor.transpose(bank[:, u, :], xwords[0, 0, g, u], ident[:])
-            nc.vector.tensor_tensor(
-                out=xm[0][0][:, g].rearrange("p r (u e) -> p r u e", u=2),
-                in0=bank[:, 0:2].bitcast(BF16).rearrange("p u (r e) -> p r u e", e=2),
-                in1=xs[:, g].rearrange("p (u e) -> p u e", u=2).unsqueeze(1).to_broadcast([P, P, 2, 2]),
-                op=ALU.mult)
-
         def x_quant(b, j0, n):
             quantize(xm[b], G * j0, G * n)
 
@@ -188,12 +178,6 @@ def tile_attentionnet_pa_kernel(tc, x_bytes, x_scale, wq, wk, out):
                                   .rearrange("r (a c i u) -> r a c u i", a=2 * G, i=2, u=2))
             for i in range(2):
                 dealt[m, f, s0 + i] = pair[:, i]
-
-        def w_deal_on_scalar(m, f, s):
-            slot = keep.tile([P, G, 2, P], F32, name=f"slot{m}{f}{s}", align_bytes=64)
-            nc.scalar.copy(out=slot[:].rearrange("r g u p -> r g p u"),
-                           in_=wraw[m, f, s].bitcast(F32).rearrange("r (g p u) -> r g p u", g=G, u=2))
-            dealt[m, f, s] = slot[:]
 
         wbank, pbank = {}, {}
 
@@ -279,9 +263,9 @@ def tile_attentionnet_pa_kernel(tc, x_bytes, x_scale, wq, wk, out):
         widen_on_vector(0, 1)
         for j in (2, 3):
             widen_plain_on_scalar(0, j)
-        x_first(0, 2)
-        x_first(1, 3)
-        warm_up(0)
+        x_turn(0, 0, 2)
+        x_scale_out(0, 0)
+        warm_up(3)
         x_turn(0, 1, 4)
         x_scale_out(0, 1)
         w_pass(K, 0, 0, 5)
@@ -290,30 +274,26 @@ def tile_attentionnet_pa_kernel(tc, x_bytes, x_scale, wq, wk, out):
         x_scale_out(0, 2)
         w_pass(K, 0, 1, 1)
         warm_up(0)
+        x_turn(0, 3, 7)
         w_pass(K, 0, 2, 2)
         w_pass(K, 0, 3, 3)
-        x_turn(0, 3, 7)
-        w_quant(K, 0, 0, 2)
-        x_quant(0, 1, 1)
-        w_quant(K, 0, 2, 2)
-        x_quant(0, 2, 1)
-        w_deal(Q, 0, 0)
         x_scale_out(0, 3)
-        w_deal(Q, 0, 2)
-        x_quant(0, 3, 1)
-        w_deal_on_scalar(K, 1, 3)
+        for s0 in (0, 2):
+            w_quant(K, 0, s0, 2)
+        x_quant(0, 1, 1)
+        x_quant(0, 2, 2)
         w_pass(K, 1, 0, 4)
         warm_up(0)
         w_pass(K, 1, 1, 5)
         w_pass(K, 1, 2, 1)
         w_pass(K, 1, 3, 2)
-        for j in range(J - 1):
-            project(K, 0, 0, j, 3 + j)
+        for j in range(J):
+            project(K, 0, 0, j, (3 + j) % 6)
         for s0 in (0, 2):
+            w_deal(Q, 0, s0)
             w_quant(K, 1, s0, 2)
         for s in range(T):
-            w_pass(Q, 0, s, s)
-        project(K, 0, 0, J - 1, 4)
+            w_pass(Q, 0, s, 1 + s)
         for first in (0, 2):
             widen_pair_on_vector(1, first)
             w_deal(Q, 1, first)

@@ -272,8 +272,8 @@ def tile_attentionnet_pa_kernel(tc, x_bytes, x_scale, wq, wk, out):
         x_turn(0, 2, 6)
         x_quant(0, 0, 1)
         x_scale_out(0, 2)
-        w_pass(K, 0, 1, 1)
         warm_up(0)
+        w_pass(K, 0, 1, 1)
         x_turn(0, 3, 7)
         w_pass(K, 0, 2, 2)
         w_pass(K, 0, 3, 3)
@@ -283,8 +283,8 @@ def tile_attentionnet_pa_kernel(tc, x_bytes, x_scale, wq, wk, out):
         x_quant(0, 1, 1)
         x_quant(0, 2, 2)
         w_pass(K, 1, 0, 4)
-        warm_up(0)
         w_pass(K, 1, 1, 5)
+        warm_up(0)
         w_pass(K, 1, 2, 1)
         w_pass(K, 1, 3, 2)
         for j in range(J):
@@ -310,10 +310,9 @@ def tile_attentionnet_pa_kernel(tc, x_bytes, x_scale, wq, wk, out):
         x_turn(1, 1, 2)
         x_scale_out(1, 0)
         w_quant(Q, 1, 0, 2)
-        p_quant(K, 0, 0, 0, 2)
         w_quant(Q, 1, 2, 2)
         x_scale_out(1, 1)
-        p_quant(K, 0, 0, 2, 2)
+        p_quant(K, 0, 0, 0, J)
         x_quant(1, 0, 2)
         x_scale_out(1, 2)
         for j in range(J):

from contextlib import ExitStack

import concourse.mybir as mybir
from concourse.masks import make_identity

B, S, D = 2, 512, 1024
SCALE = 128.0 ** -0.5
FLOPS = 2 * 2 * B * S * D * D + 2 * B * S * S * D

F32 = mybir.dt.float32
BF16 = mybir.dt.bfloat16
U32 = mybir.dt.uint32
U8 = mybir.dt.uint8
FP8 = mybir.dt.float8_e4m3fn
FP8X4 = mybir.dt.float8_e4m3fn_x4
ALU = mybir.AluOpType
ACT = mybir.ActivationFunctionType

P = 128
G = 2
T = 4
J = 4
F = 2
K, Q = 0, 1
BANK = 512
FIRST_WARM_UP = 224
LAST_ON_VECTOR = 352


def tile_attentionnet_pa_kernel(tc, x_bytes, x_scale, wq, wk, out):
    nc = tc.nc
    with ExitStack() as ctx:
        keep = ctx.enter_context(tc.tile_pool(name="keep", bufs=1))
        stage = ctx.enter_context(tc.tile_pool(name="stage", bufs=4))
        soft = ctx.enter_context(tc.tile_pool(name="soft", bufs=4))
        psum = ctx.enter_context(tc.psum_pool(name="psum", bufs=8))
        ctx.enter_context(tc.manual_schedule())

        xs = keep.tile([P, G, T], F32, name="xs")
        xraw, xpair, wraw, wload = {}, {}, {}, {}

        def load_x(b, j0, n):
            raw = keep.tile([P, n, D], U8, name=f"xraw{b}{j0}")
            nc.sync.dma_start(out=raw[:], in_=x_bytes[b].rearrange("(h r i) k -> h r i k", h=2, i=2)[j0 // 2, :, j0 % 2:j0 % 2 + n, :])
            for i in range(n):
                xraw[b, j0 + i] = raw[:, i, :]
            for i in range(0, n - 1, 2):
                xpair[b, j0 + i] = raw[:, i:i + 2, :]

        def load_w(m, f, s0, n):
            raw = keep.tile([P, n, D], BF16, name=f"wraw{m}{f}{s0}", align_bytes=64)
            rows = (wk, wq)[m][f * 512:(f + 1) * 512, :].rearrange("(m t) k -> m t k", t=T)
            nc.sync.dma_start(out=raw[:], in_=rows[:, s0:s0 + n, :])
            wload[m, f, s0] = raw
            for i in range(n):
                wraw[m, f, s0 + i] = raw[:, i, :]

        load_x(0, 0, 1)
        nc.scalar.dma_start(out=xs[:], in_=x_scale.rearrange("o i (g p t) -> p (o i g) t", g=G, t=T))
        load_x(0, 1, 1)
        load_x(0, 2, 2)
        load_w(K, 0, 0, 1)
        load_w(K, 0, 1, 1)
        load_w(K, 0, 2, 2)
        for m, f in ((K, 1), (Q, 0)):
            for s0 in (0, 2):
                load_w(m, f, s0, 2)
        for j0 in (0, 2):
            load_x(1, j0, 2)
        for s0 in (0, 2):
            load_w(Q, 1, s0, 2)

        zero = keep.tile([P, BANK // 2], F32, name="zero")
        nc.gpsimd.memset(zero[:], 0.0)
        ident = keep.tile([P, P], F32, name="ident")
        nc.vector.memset(ident[:], 0.0)
        make_identity(nc, ident[:], nomemset=True)
        warm = keep.tile([P, 1], F32, name="warm")
        nc.scalar.activation(out=warm[:], in_=zero[:, 0:1], func=ACT.Exp)

        def mx_tiles(name, rows):
            return (keep.tile([P, rows, P, T], BF16, name=name + "v", align_bytes=64),
                    keep.tile([P, rows, P], U32, name=name + "c", align_bytes=64),
                    keep.tile([P, rows, P], U8, name=name + "s", align_bytes=64))

        xm = [mx_tiles(f"x{b}", J * G) for b in range(B)]
        wm = {(m, f): mx_tiles(f"w{m}{f}", T * G) for m in (K, Q) for f in range(F)}
        pm = {(m, b): mx_tiles(f"p{m}{b}", F * J) for m in (K, Q) for b in range(B)}

        def p_row(m, f, j):
            return J * f + j if m == K else F * j + f

        def quantize(tiles, first, n):
            values, codes, scales = (tile[:, first:first + n] for tile in tiles)
            nc.vector.quantize_mx(out=codes.rearrange("p a r -> p (a r)").bitcast(FP8X4),
                                  scales=scales.rearrange("p a r -> p (a r)"),
                                  in_=values.rearrange("p a r t -> p (a r t)"))

        def operand(tiles, first, n=1):
            return (tiles[1][:, first:first + n].rearrange("p a r -> p (a r)").bitcast(FP8X4),
                    tiles[2][:, first:first + n].rearrange("p a r -> p (a r)"))

        def new_bank(n):
            return psum.tile([P, T, P], F32, name=f"bank{n}", bufs=1)

        def every_second(pairs, g, u):
            return pairs[:, 256 * g + u:256 * (g + 1):2]

        def first_warm_up(n):
            nc.tensor.matmul(new_bank(n)[:].rearrange("p t n -> p (t n)")[:, 0:FIRST_WARM_UP],
                             lhsT=zero[:, 0:P], rhs=zero[:, 0:FIRST_WARM_UP], start=True, stop=True)

        def warm_up(n):
            zero16 = zero[:].bitcast(BF16)
            nc.tensor.matmul(new_bank(n)[:].rearrange("p t n -> p (t n)"),
                             lhsT=zero16[:, 0:P], rhs=zero16[:, 0:BANK], start=True, stop=True)

        xwords, xbank = {}, {}

        def widen_on_vector(b, j):
            wide = stage.tile([P, 2, G * P, 2], BF16, name="wide", align_bytes=64)
            nc.vector.tensor_copy(out=wide[:].rearrange("r u c e -> r c u e"),
                                  in_=xraw[b, j].bitcast(FP8).rearrange("r (c u e) -> r c u e", u=2, e=2))
            for g in range(G):
                for u in range(2):
                    xwords[b, j, g, u] = wide[:, u, g * P:(g + 1) * P].rearrange("r p e -> r (p e)").bitcast(F32)

        def widen_pair_on_vector(b, j0):
            wide = stage.tile([P, 2, 2 * G * P, 2], BF16, name="wide2", bufs=2, align_bytes=64)
            nc.vector.tensor_copy(out=wide[:].rearrange("r u c e -> r c u e"),
                                  in_=xpair[b, j0].rearrange("r j k -> r (j k)").bitcast(FP8)
                                    .rearrange("r (c u e) -> r c u e", u=2, e=2))
            for a in range(2 * G):
                for u in range(2):
                    xwords[b, j0 + a // G, a % G, u] = (wide[:, u, a * P:(a + 1) * P]
                                                        .rearrange("r p e -> r (p e)").bitcast(F32))

        def widen_halves(b, j):
            codes = xraw[b, j].bitcast(FP8)
            first = stage.tile([P, 2, P, 2], BF16, name="first_half", bufs=1, align_bytes=64)
            nc.vector.tensor_copy(out=first[:].rearrange("r u c e -> r c u e"),
                                  in_=codes[:, 0:512].rearrange("r (c u e) -> r c u e", u=2, e=2))
            second = stage.tile([P, 512], BF16, name="second_half", bufs=1, align_bytes=64)
            nc.scalar.copy(out=second[:], in_=codes[:, 512:1024])
            for u in range(2):
                xwords[b, j, 0, u] = first[:, u].rearrange("r p e -> r (p e)").bitcast(F32)
                xwords[b, j, 1, u] = every_second(second[:].bitcast(F32), 0, u)

        def widen_plain_on_scalar(b, j):
            wide = stage.tile([P, D], BF16, name="wide", align_bytes=64)
            nc.scalar.copy(out=wide[:], in_=xraw[b, j].bitcast(FP8))
            for g in range(G):
                for u in range(2):
                    xwords[b, j, g, u] = every_second(wide[:].bitcast(F32), g, u)

        def x_turn(b, j, n):
            xbank[b, j] = new_bank(n)
            for g in range(G):
                for u in range(2):
                    nc.tensor.transpose(xbank[b, j][:, G * u + g, :], xwords[b, j, g, u], ident[:])

        def x_scale_out(b, j):
            nc.vector.tensor_tensor(
                out=xm[b][0][:, G * j:G * (j + 1)].rearrange("p g r (u e) -> p g r u e", u=2),
                in0=xbank[b, j][:].bitcast(BF16).rearrange("p (u g) (r e) -> p g r u e", u=2, e=2),
                in1=xs[:].rearrange("p g (u e) -> p g u e", u=2).unsqueeze(2).to_broadcast([P, G, P, 2, 2]),
                op=ALU.mult)

        def x_quant(b, j0, n):
            quantize(xm[b], G * j0, G * n)

        dealt = {}

        def w_deal(m, f, s0):
            pair = stage.tile([P, 2, G, 2, P], F32, name="dealt", bufs=2, align_bytes=64)
            nc.vector.tensor_copy(out=pair[:].rearrange("r s g u (c i) -> r (s g) c u i", i=2),
                                  in_=wload[m, f, s0][:].rearrange("r s k -> r (s k)").bitcast(F32)
                                  .rearrange("r (a c i u) -> r a c u i", a=2 * G, i=2, u=2))
            for i in range(2):
                dealt[m, f, s0 + i] = pair[:, i]

        wbank, pbank = {}, {}

        def w_turn(m, f, s, n):
            bank = wbank[m, f, s] = new_bank(n)
            for g in range(G):
                for u in range(2):
                    if (m, f, s) in dealt:
                        view = dealt[m, f, s][:, g, u, :]
                    else:
                        view = every_second(wraw[m, f, s].bitcast(F32), g, u)
                    nc.tensor.transpose(bank[:, 2 * g + u, :], view, ident[:])

        def w_copy(m, f, s):
            nc.scalar.copy(out=wm[m, f][0][:, G * s:G * (s + 1)].bitcast(F32),
                           in_=wbank[m, f, s][:].rearrange("p (g u) r -> p g r u", u=2))

        def w_quant(m, f, s0, n):
            quantize(wm[m, f], G * s0, G * n)

        def p_mul(m, f, b, j, n):
            bank = pbank[m, f, b, j] = new_bank(n)
            for s in range(T):
                for g in range(G):
                    wc, wsc = operand(wm[m, f], G * s + g)
                    xc, xsc = operand(xm[b], G * j + g)
                    nc.tensor.matmul_mx(out=bank[:, s, :], lhsT=wc, lhsT_scale=wsc, rhs=xc, rhs_scale=xsc,
                                        start=(g == 0), stop=(g == G - 1))

        def p_copy(m, f, b, j):
            nc.scalar.copy(out=pm[m, b][0][:, p_row(m, f, j)], in_=pbank[m, f, b, j][:].rearrange("p t n -> p n t"))

        def project(m, f, b, j, n):
            p_mul(m, f, b, j, n)
            p_copy(m, f, b, j)

        def w_pass(m, f, s, n):
            w_turn(m, f, s, n)
            w_copy(m, f, s)

        def p_quant(m, f, b, j, n):
            quantize(pm[m, b], p_row(m, f, j), n)

        sbank, scaled, nbias, e, tot, inv = {}, {}, {}, {}, {}, {}

        def scores(b, j, n):
            sbank[b, j] = new_bank(n)
            for f in range(F):
                qc, qsc = operand(pm[Q, b], p_row(Q, f, j))
                kc, ksc = operand(pm[K, b], p_row(K, f, 0), J)
                nc.tensor.matmul_mx(out=sbank[b, j][:].rearrange("p j r -> p (j r)"), lhsT=qc, lhsT_scale=qsc,
                                    rhs=kc, rhs_scale=ksc, start=(f == 0), stop=(f == F - 1))

        def row_bias(b, j):
            nbias[b, j] = soft.tile([P, 1], F32, name="nbias")
            scaled[b, j] = soft.tile([P, 2, P, 2], F32, name="scaled", bufs=3)
            nc.vector.tensor_scalar(out=scaled[b, j][:], in0=sbank[b, j][:].rearrange("p (h i) r -> p h r i", i=2), scalar1=-SCALE,
                                    scalar2=None, op0=ALU.mult, op1=ALU.min, accum_out=nbias[b, j][:])

        def row_exp(b, j):
            e[b, j] = soft.tile([P, 2, P, 2], F32, name="e")
            tot[b, j] = soft.tile([P, 1], F32, name="tot")
            nc.scalar.activation(out=e[b, j][:], in_=scaled[b, j][:], func=ACT.Exp,
                                 bias=nbias[b, j][:], scale=-1.0, accum_out=tot[b, j][:])

        def row_inv(b, j):
            inv[b, j] = soft.tile([P, 1], F32, name="inv")
            nc.vector.reciprocal(out=inv[b, j][:], in_=tot[b, j][:])

        def row_out(b, j, on_vector=S):
            prob = soft.tile([P, S], F32, name="prob", bufs=5)
            rows = e[b, j][:].rearrange("p h r i -> p (h r i)")
            if on_vector > 0:
                nc.vector.tensor_scalar(out=prob[:, :on_vector], in0=rows[:, :on_vector], scalar1=inv[b, j][:],
                                        scalar2=None, op0=ALU.mult)
            if on_vector < S:
                nc.scalar.activation(out=prob[:, on_vector:], in_=rows[:, on_vector:], func=ACT.Copy, scale=inv[b, j][:])
            nc.sync.dma_start(out=out[b].rearrange("(h r i) s -> h i r s", h=2, i=2)[j // 2, j % 2], in_=prob[:])

        first_warm_up(0)
        first_warm_up(1)
        widen_halves(0, 0)
        widen_on_vector(0, 1)
        for j in (2, 3):
            widen_plain_on_scalar(0, j)
        x_turn(0, 0, 2)
        x_scale_out(0, 0)
        warm_up(3)
        x_turn(0, 1, 4)
        x_scale_out(0, 1)
        w_pass(K, 0, 0, 5)
        x_turn(0, 2, 6)
        x_quant(0, 0, 1)
        x_scale_out(0, 2)
        warm_up(0)
        w_pass(K, 0, 1, 1)
        x_turn(0, 3, 7)
        w_pass(K, 0, 2, 2)
        w_pass(K, 0, 3, 3)
        x_scale_out(0, 3)
        for s0 in (0, 2):
            w_quant(K, 0, s0, 2)
        x_quant(0, 1, 1)
        x_quant(0, 2, 2)
        w_pass(K, 1, 0, 4)
        w_pass(K, 1, 1, 5)
        warm_up(0)
        w_pass(K, 1, 2, 1)
        w_pass(K, 1, 3, 2)
        for j in range(J):
            project(K, 0, 0, j, (3 + j) % 6)
        for s0 in (0, 2):
            w_deal(Q, 0, s0)
            w_quant(K, 1, s0, 2)
        for s in range(T):
            w_pass(Q, 0, s, 1 + s)
        for first in (0, 2):
            widen_pair_on_vector(1, first)
            w_deal(Q, 1, first)
        for j in range(J):
            project(K, 1, 0, j, (5 + j) % 6)
        w_quant(Q, 0, 0, T)
        w_pass(Q, 1, 0, 3)
        w_pass(Q, 1, 1, 4)
        x_turn(1, 0, 5)
        x_turn(1, 2, 6)
        x_turn(1, 3, 7)
        w_pass(Q, 1, 2, 0)
        w_pass(Q, 1, 3, 1)
        x_turn(1, 1, 2)
        x_scale_out(1, 0)
        w_quant(Q, 1, 0, 2)
        w_quant(Q, 1, 2, 2)
        x_scale_out(1, 1)
        p_quant(K, 0, 0, 0, J)
        x_quant(1, 0, 2)
        x_scale_out(1, 2)
        for j in range(J):
            project(Q, 0, 0, j, (3 + j) % 6)
        ring = (5, 0, 1, 3, 4, 2)
        for j in range(J):
            project(Q, 1, 0, j, ring[2 + j])
        p_quant(K, 1, 0, 0, J)
        p_quant(Q, 0, 0, 0, F)
        x_quant(1, 2, 1)
        x_scale_out(1, 3)
        p_quant(Q, 0, 0, 1, F)
        x_quant(1, 3, 1)
        tiles = [(b, j) for b in range(B) for j in range(J)]
        for i in range(2 * J):
            m, j = (K, i) if i < J else (Q, i - J)
            last = i == 2 * J - 1
            project(m, 0, 1, j, ring[2 * i % 6])
            if last:
                p_quant(Q, 0, 1, j, 1)
            project(m, 1, 1, j, ring[(2 * i + 1) % 6])
            if i >= 2:
                row_exp(*tiles[i - 2])
            if last:
                p_quant(Q, 1, 1, j, 1)
            elif m == Q:
                p_quant(Q, 0, 1, j, F)
            if i >= 1:
                scores(*tiles[i - 1], 7 - i % 2)
                row_bias(*tiles[i - 1])
            if i in (1, 2):
                p_quant(Q, 0, 0, i + 1, F)
            if m == K and i % 2 == 1:
                for f in range(F):
                    p_quant(K, f, 1, i - 1, 2)
            if i >= 2:
                row_inv(*tiles[i - 2])
            if 3 <= i < 7:
                row_out(*tiles[i - 3])
        scores(1, 3, ring[4])
        row_out(1, 0, 0)
        row_exp(1, 2)
        row_bias(1, 3)
        row_exp(1, 3)
        row_out(1, 1)
        for j in (2, 3):
            row_inv(1, j)
            row_out(1, j, LAST_ON_VECTOR if j == J - 1 else S)
